import numpy as np
import ml_dtypes


def mxq(x, axis, fmt="e4m3"):
    dtype, down = {"e4m3": (ml_dtypes.float8_e4m3fn, 7), "e5m2": (ml_dtypes.float8_e5m2, 14)}[fmt]
    v = np.moveaxis(np.asarray(x, np.float32).astype(ml_dtypes.bfloat16).astype(np.float64), axis, -1)
    blocks = v.reshape(v.shape[:-1] + (-1, 32))
    amax = np.abs(blocks).max(-1, keepdims=True)
    byte = np.maximum(np.where(amax > 0, np.frexp(amax)[1] - 1 + 127, 0) - down, 1)
    scale = np.exp2(byte - 127.0)
    codes = (blocks / scale).astype(np.float32).astype(dtype).astype(np.float64)
    return np.moveaxis((codes * scale).reshape(v.shape), -1, axis)


WIDE = False


def mx_kscale(k):
    if not WIDE:
        return np.ones(k)
    levels = np.array([10, -10, 5, -5, 0])
    a = np.random.permutation(np.resize(levels, k // 512 * 4)).reshape(k // 512, 4)
    idx = np.arange(k)
    return np.exp2(a[idx // 512, idx % 128 // 32])


BF16 = ml_dtypes.bfloat16


def bf(x):
    return np.asarray(x, np.float32).astype(BF16)


def f64(x):
    return np.asarray(x).astype(np.float64)


B, S, DIM, HEADS, DH = 1, 128, 512, 4, 128
HD = HEADS * DH
FILL = 1e-6
V_RMS, V_MEAN = 10.0, 4.0


def setup_inputs():
    t = mx_kscale(HD)
    offset = V_MEAN * np.sign(np.random.standard_normal((HEADS, 1, DH))) * (1.0 + 0.2 * np.random.standard_normal((HEADS, 1, DH)))
    return {
        "a_heads": bf(np.random.standard_normal((S, HEADS, DH))),
        "step2": bf(np.random.standard_normal((S, DH, S)) * 0.5 * np.sqrt(HD)),
        "v_pairs": bf((np.random.standard_normal((HEADS, S * S, DH)) * V_RMS + offset) * t.reshape(HEADS, 1, DH)),
        "W_out": bf(np.random.standard_normal((DIM, HD)) * 0.5 / np.sqrt(HD) / t),
        "b_out": bf(0.1 * np.random.standard_normal(DIM)),
    }


def reference(a_heads, step2, v_pairs, W_out, b_out):
    a2 = f64(a_heads).transpose(1, 0, 2).reshape(HEADS * S, DH)
    s = (a2 @ f64(step2)).reshape(S, HEADS, S, S)
    p_idx = np.arange(S)[:, None]
    q_idx = np.arange(S)[None, :]
    s = np.where(p_idx >= q_idx, FILL, s)
    s = s.transpose(1, 0, 2, 3).reshape(HEADS, S, S * S) / DH
    e = np.exp(s - s.max(-1, keepdims=True))
    z = (mxq(e, 2, "e4m3") @ mxq(f64(v_pairs), 1, "e4m3")) / e.sum(-1, keepdims=True)
    z = z.transpose(1, 0, 2).reshape(S, HD)
    return (mxq(z, 1, "e4m3") @ mxq(f64(W_out), 1, "e4m3").T) + f64(b_out)

@@ -1,0 +1,325 @@
+from contextlib import ExitStack
+
+import concourse.mybir as mybir
+from concourse.masks import make_identity
+
+F32 = mybir.dt.float32
+BF16 = mybir.dt.bfloat16
+U32 = mybir.dt.uint32
+U8 = mybir.dt.uint8
+FP8X4 = mybir.dt.float8_e4m3fn_x4
+ALU = mybir.AluOpType
+ACT = mybir.ActivationFunctionType
+AX = mybir.AxisListType
+
+P = 128
+HEADS = 4
+FILL = 1e-6
+INV_DH = 1.0 / 128.0
+N_MASKED = 128 * 129 // 2
+ROWS = 64
+QUADS = 8
+GROUP = 4
+
+CHUNK_MASKED = ((64, 0), (64, 32))
+CHUNK_DIAG_A = ((0, 0), (64, 64))
+CHUNK_DIAG_B = ((0, 32), (64, 96))
+CHUNK_LIVE = ((0, 64), (0, 96))
+CHUNKS = (CHUNK_MASKED, CHUNK_DIAG_A, CHUNK_DIAG_B, CHUNK_LIVE)
+
+ER_WIDTH = GROUP * 512 + 256
+
+FLOPS = 2 * 128 * 512 * 128 * 128 + 2 * 4 * 128 * 16384 * 128 + 2 * 128 * 512 * 512
+
+
+def rows_below_diagonal(chunk, quad):
+    p0, q0 = chunk[0]
+    return min(ROWS, max(0, q0 - p0 + 4 * quad))
+
+
+def tile_trittentioncube_pb_kernel(tc, a_heads, step2, v_pairs, W_out, b_out, out):
+    nc = tc.nc
+    v_plane = v_pairs.rearrange("n (p q) f -> n p q f", q=P)
+
+    with ExitStack() as stack:
+        keep = stack.enter_context(tc.tile_pool(name="keep", bufs=1))
+
+        ident_bf = keep.tile([P, P], BF16)
+        make_identity(nc, ident_bf)
+        ident_f32 = keep.tile([P, P], F32)
+        make_identity(nc, ident_f32)
+
+        a_t = keep.tile([P, HEADS, P], BF16)
+        s2 = keep.tile([P, P, P], BF16)
+        w_codes = keep.tile([P, 512], U32, align_bytes=64)
+        w_scales = keep.tile([P, 512], U8, align_bytes=64)
+        bias_rows = keep.tile([P, 512], BF16)
+        v_codes = keep.tile([P, HEADS, len(CHUNKS), QUADS, P], U32, align_bytes=64)
+        v_scales = keep.tile([P, HEADS, len(CHUNKS), QUADS, P], U8, align_bytes=64)
+        part_max = keep.tile([P, P, HEADS], F32)
+        top = keep.tile([P, HEADS], F32)
+        neg_m = keep.tile([P, HEADS], F32)
+        e_fill = keep.tile([P, HEADS], F32)
+        live01 = keep.tile([P, 32], F32)
+        mask01 = keep.tile([P, 32], F32)
+        diag_e = keep.tile([P, HEADS, 512], F32)
+        diag_sum = keep.tile([P, HEADS], F32)
+        diag_bf = keep.tile([P, HEADS, 512], BF16)
+        sums = keep.tile([P, HEADS, 24], F32)
+        total = keep.tile([P, HEADS], F32)
+        recip = keep.tile([P, HEADS], F32)
+        z_bf = keep.tile([P, HEADS * P], BF16)
+
+        with tc.tile_pool(name="early", bufs=1) as early, tc.psum_pool(name="ps_early", bufs=1) as ps_early:
+            a_rows = early.tile([P, HEADS * P], BF16)
+            nc.sync.dma_start(out=a_rows, in_=a_heads.rearrange("p n i -> p (n i)"))
+            s_raw = early.tile([P, P, P], BF16)
+            for rc in range(8):
+                r_cols = slice(16 * rc, 16 * rc + 16)
+                nc.sync.dma_start(out=s_raw[:, r_cols, :], in_=step2[r_cols].rearrange("r i q -> i r q"))
+            w_rows = early.tile([P, 4, 512], BF16)
+            nc.sync.dma_start(out=w_rows, in_=W_out.rearrange("(c o) k -> o c k", o=P))
+            nc.sync.dma_start(out=bias_rows, in_=b_out.partition_broadcast(P))
+
+            a_ps = ps_early.tile([P, HEADS, P], BF16)
+            for n in range(HEADS):
+                nc.tensor.transpose(a_ps[:, n, :], a_rows[:, n * P : (n + 1) * P], ident_bf)
+            nc.vector.tensor_copy(out=a_t, in_=a_ps)
+
+            for rc in range(8):
+                r_cols = slice(16 * rc, 16 * rc + 16)
+                src = s_raw[:, r_cols, :].rearrange("i r q -> i q r")
+                if rc % 2 == 0:
+                    nc.vector.tensor_copy(out=s2[:, :, r_cols], in_=src)
+                elif rc % 4 == 1:
+                    nc.scalar.copy(out=s2[:, :, r_cols], in_=src)
+                else:
+                    nc.gpsimd.tensor_scalar(
+                        out=s2[:, :, r_cols], in0=src, scalar1=1.0, scalar2=0.0, op0=ALU.mult, op1=ALU.add
+                    )
+
+            nc.vector.memset(part_max[:, 0, :], FILL)
+            for q in range(1, P):
+                s_ps = ps_early.tile([P, HEADS, P], F32, bufs=4)
+                nc.tensor.matmul(out=s_ps[:, :, 0:q], lhsT=s2[:, q, :], rhs=a_t[:, :, 0:q], start=True, stop=True)
+                nc.vector.tensor_reduce(out=part_max[:, q, :], in_=s_ps[:, :, 0:q], axis=AX.X, op=ALU.max)
+            nc.vector.tensor_reduce(out=top, in_=part_max.rearrange("r q n -> r n q"), axis=AX.X, op=ALU.max)
+            nc.vector.tensor_scalar(out=neg_m, in0=top, scalar1=-INV_DH, scalar2=None, op0=ALU.mult)
+            nc.scalar.activation(out=e_fill, in_=neg_m, func=ACT.Exp, bias=FILL * INV_DH, scale=1.0)
+
+            w_words = w_rows.bitcast(F32)
+            w_grouped = early.tile([P, 2048], BF16, align_bytes=64)
+            w_grouped_words = w_grouped.bitcast(F32).rearrange("x (c o u) -> x c o u", c=4, u=2)
+            for half in range(2):
+                w_ps = ps_early.tile([P, 2, 2, P], F32, bufs=2)
+                for c in range(2):
+                    for u in range(2):
+                        nc.tensor.transpose(w_ps[:, c, u, :], w_words[:, 2 * half + c, u * P : (u + 1) * P], ident_f32)
+                nc.vector.tensor_copy(
+                    out=w_grouped_words[:, 2 * half : 2 * half + 2], in_=w_ps.rearrange("x c u o -> x c o u")
+                )
+            nc.vector.quantize_mx(out=w_codes.bitcast(FP8X4), scales=w_scales, in_=w_grouped)
+
+        stream = stack.enter_context(tc.tile_pool(name="stream", bufs=3))
+        e_pool = stack.enter_context(tc.tile_pool(name="e_pool", bufs=2))
+        ps_s = stack.enter_context(tc.psum_pool(name="ps_s", bufs=3))
+        ps_t = stack.enter_context(tc.psum_pool(name="ps_t", bufs=2))
+        ps_z = stack.enter_context(tc.psum_pool(name="ps_z", bufs=2))
+        ps_o = stack.enter_context(tc.psum_pool(name="ps_o", bufs=1))
+
+        live_cells = live01.rearrange("r (u j h e) -> r u j h e", u=2, j=4, h=2)
+        nc.vector.memset(live01, 0.0)
+        for t in range(1, 4):
+            nc.vector.memset(live_cells[:, t // 2, 0:t, :, t % 2], 1.0)
+        nc.vector.tensor_scalar(out=mask01, in0=live01, scalar1=-1.0, scalar2=1.0, op0=ALU.mult, op1=ALU.add)
+        nc.vector.memset(sums, 0.0)
+
+        for bank in range(4):
+            d_ps = ps_s.tile([P, 512], F32, name="s_ps")
+            d_cells = d_ps.rearrange("r (n s u j h e) -> r n s u j h e", n=HEADS, s=4, u=2, j=4, h=2)
+            for s_in in range(4):
+                s = 4 * bank + s_in
+                for h in range(2):
+                    corner = 64 * h + 4 * s
+                    for t in range(4):
+                        nc.tensor.matmul(
+                            out=d_cells[:, :, s_in, t // 2, :, h, t % 2],
+                            lhsT=s2[:, corner + t, :],
+                            rhs=a_t[:, :, corner : corner + 4],
+                            start=True,
+                            stop=True,
+                        )
+            for n in range(HEADS):
+                nc.scalar.activation(
+                    out=diag_e[:, n, bank * P : (bank + 1) * P],
+                    in_=d_ps[:, n * P : (n + 1) * P],
+                    func=ACT.Exp,
+                    bias=neg_m[:, n : n + 1],
+                    scale=INV_DH,
+                )
+        nc.vector.tensor_tensor(
+            out=diag_e.rearrange("r n (s x) -> r (n s) x", x=32),
+            in0=diag_e.rearrange("r n (s x) -> r (n s) x", x=32),
+            in1=live01.unsqueeze(1).to_broadcast([P, HEADS * 16, 32]),
+            op=ALU.min,
+        )
+        nc.vector.tensor_reduce(out=diag_sum, in_=diag_e, axis=AX.X, op=ALU.add)
+        for n in range(HEADS):
+            nc.vector.scalar_tensor_tensor(
+                out=diag_bf[:, n, :].rearrange("r (s x) -> r s x", x=32),
+                in0=mask01.unsqueeze(1).to_broadcast([P, 16, 32]),
+                scalar=e_fill[:, n : n + 1],
+                in1=diag_e[:, n, :].rearrange("r (s x) -> r s x", x=32),
+                op0=ALU.mult,
+                op1=ALU.add,
+            )
+
+        def load_and_quantise_v(n, ci):
+            raw = stream.tile([P, 4 * QUADS, P], BF16)
+            for h, (p0, q0) in enumerate(CHUNKS[ci]):
+                nc.sync.dma_start(out=raw[h:P:2, :, :], in_=v_plane[n, p0 : p0 + ROWS, q0 : q0 + 4 * QUADS, :])
+            grouped = stream.tile([P, QUADS, P, 4], BF16, align_bytes=64)
+            nc.vector.tensor_copy(
+                out=grouped[:, 0:4].rearrange("x j (c i) t -> x j c t i", i=4),
+                in_=raw[:, 0:16, :].rearrange("x (j t) (c i) -> x j c t i", t=4, i=4),
+            )
+            nc.scalar.copy(out=grouped[:, 4:8], in_=raw[:, 16:32, :].rearrange("x (j t) f -> x j f t", t=4))
+            nc.vector.quantize_mx(
+                out=v_codes[:, n, ci].rearrange("x j f -> x (j f)").bitcast(FP8X4),
+                scales=v_scales[:, n, ci].rearrange("x j f -> x (j f)"),
+                in_=grouped.rearrange("x j f t -> x (j f t)"),
+            )
+
+        def scores_and_exp(n, chunk, quad, e_rows, sum_col):
+            rows = rows_below_diagonal(chunk, quad)
+            s_ps = ps_s.tile([P, 512], F32)
+            cells = s_ps[:, 0 : 8 * rows].rearrange("r (u p h e) -> r u p h e", u=2, h=2, e=2)
+            for h, (p0, q0) in enumerate(chunk):
+                for t in range(4):
+                    nc.tensor.matmul(
+                        out=cells[:, t // 2, :, h, t % 2],
+                        lhsT=s2[:, q0 + 4 * quad + t, :],
+                        rhs=a_t[:, n, p0 : p0 + rows],
+                        start=True,
+                        stop=True,
+                    )
+            nc.scalar.activation(
+                out=e_rows[:, :, 0 : 4 * rows],
+                in_=s_ps[:, 0 : 8 * rows].rearrange("r (u x) -> r u x", u=2),
+                func=ACT.Exp,
+                bias=neg_m[:, n : n + 1],
+                scale=INV_DH,
+                accum_out=sums[:, n, sum_col : sum_col + 1],
+            )
+
+        def transpose_and_quantise(e_words, passes):
+            grouped = e_pool.tile([P, GROUP * 512], BF16, align_bytes=64, name="e_grouped")
+            grouped_words = grouped.bitcast(F32).rearrange("x (g r u) -> x g r u", g=GROUP, u=2)
+            for first in range(0, passes, 2):
+                pair = min(2, passes - first)
+                t_ps = ps_t.tile([P, 2, 2, P], F32)
+                for g in range(pair):
+                    for u in range(2):
+                        start_word = 256 * (first + g) + P * u
+                        nc.tensor.transpose(t_ps[:, g, u, :], e_words[:, start_word : start_word + P], ident_f32)
+                copy_out = nc.scalar.copy if first % 4 == 0 else nc.vector.tensor_copy
+                copy_out(
+                    out=grouped_words[:, first : first + pair],
+                    in_=t_ps[:, 0:pair].rearrange("x g u r -> x g r u"),
+                )
+            codes = e_pool.tile([P, GROUP * P], U32, align_bytes=64, name="e_codes")
+            scales = e_pool.tile([P, GROUP * P], U8, align_bytes=64, name="e_scales")
+            nc.vector.quantize_mx(
+                out=codes[:, 0 : passes * P].bitcast(FP8X4),
+                scales=scales[:, 0 : passes * P],
+                in_=grouped[:, 0 : passes * 512],
+            )
+            return codes, scales
+
+        def multiply(z_ps, n, codes, scales, g, ci, quad):
+            nc.tensor.matmul_mx(
+                out=z_ps,
+                lhsT=codes[:, g * P : (g + 1) * P].bitcast(FP8X4),
+                lhsT_scale=scales[:, g * P : (g + 1) * P],
+                rhs=v_codes[:, n, ci, quad, :].bitcast(FP8X4),
+                rhs_scale=v_scales[:, n, ci, quad, :],
+                start=(ci == 0 and quad == 0),
+                stop=(ci == len(CHUNKS) - 1 and quad == QUADS - 1),
+            )
+
+        for n in range(HEADS):
+            for ci in range(len(CHUNKS)):
+                load_and_quantise_v(n, ci)
+
+            z_ps = ps_z.tile([P, P], F32)
+
+            e_const = e_pool.tile([P, 512], BF16)
+            nc.gpsimd.tensor_scalar(
+                out=e_const, in0=e_fill[:, n : n + 1].to_broadcast([P, 512]),
+                scalar1=1.0, scalar2=0.0, op0=ALU.mult, op1=ALU.add,
+            )
+            e_diag = []
+            for half in range(2):
+                e_tile = e_pool.tile([P, ER_WIDTH], BF16, name="e_diag%d" % half)
+                nc.gpsimd.tensor_scalar(
+                    out=e_tile[:, 0 : GROUP * 512], in0=e_fill[:, n : n + 1].to_broadcast([P, GROUP * 512]),
+                    scalar1=1.0, scalar2=0.0, op0=ALU.mult, op1=ALU.add,
+                )
+                e_diag.append(e_tile)
+
+            codes, scales = transpose_and_quantise(e_const.bitcast(F32), 1)
+            for quad in range(QUADS):
+                multiply(z_ps, n, codes, scales, 0, 0, quad)
+
+            for ci in (1, 2, 3):
+                chunk = CHUNKS[ci]
+                for half in range(2):
+                    on_diagonal = ci < 3
+                    if on_diagonal:
+                        e_tile = e_diag[half]
+                    else:
+                        e_tile = e_pool.tile([P, GROUP * 512], BF16, name="e_live")
+                    for g in range(GROUP):
+                        quad = GROUP * half + g
+                        if rows_below_diagonal(chunk, quad) > 0:
+                            scores_and_exp(
+                                n, chunk, quad,
+                                e_tile[:, 512 * g : 512 * (g + 1)].rearrange("r (u x) -> r u x", u=2),
+                                QUADS * (ci - 1) + quad,
+                            )
+                    if on_diagonal:
+                        s0 = rows_below_diagonal(chunk, GROUP * half) // 4
+                        nc.vector.tensor_copy(
+                            out=e_tile[:, 16 * s0 : 16 * s0 + GROUP * 528]
+                            .rearrange("r (g y) -> r g y", y=528)[:, :, 0:512]
+                            .rearrange("r g (u x) -> r g u x", u=2)[:, :, :, 0:16],
+                            in_=diag_bf[:, n, 32 * s0 : 32 * (s0 + GROUP)].rearrange("r (g u x) -> r g u x", g=GROUP, u=2),
+                        )
+                    codes, scales = transpose_and_quantise(e_tile.bitcast(F32), GROUP)
+                    for g in range(GROUP):
+                        multiply(z_ps, n, codes, scales, g, ci, GROUP * half + g)
+
+            one = slice(n, n + 1)
+            nc.vector.tensor_reduce(out=total[:, one], in_=sums[:, n, :], axis=AX.X, op=ALU.add)
+            nc.vector.tensor_tensor(out=total[:, one], in0=total[:, one], in1=diag_sum[:, one], op=ALU.add)
+            nc.vector.scalar_tensor_tensor(
+                out=total[:, one], in0=e_fill[:, one], scalar=float(N_MASKED), in1=total[:, one],
+                op0=ALU.mult, op1=ALU.add,
+            )
+            nc.vector.reciprocal(out=recip[:, one], in_=total[:, one])
+            nc.scalar.activation(out=z_bf[:, n * P : (n + 1) * P], in_=z_ps, func=ACT.Copy, scale=recip[:, one])
+
+        z_codes, z_scales = transpose_and_quantise(z_bf.bitcast(F32), 1)
+        o_ps = ps_o.tile([P, 512], F32)
+        nc.tensor.matmul_mx(
+            out=o_ps,
+            lhsT=z_codes[:, 0:P].bitcast(FP8X4),
+            lhsT_scale=z_scales[:, 0:P],
+            rhs=w_codes.bitcast(FP8X4),
+            rhs_scale=w_scales,
+            start=True,
+            stop=True,
+        )
+        o_sb = keep.tile([P, 512], F32)
+        nc.vector.tensor_tensor(out=o_sb, in0=o_ps, in1=bias_rows, op=ALU.add)
+        nc.sync.dma_start(out=out, in_=o_sb)

@@ -16,30 +16,36 @@ P = 128
 HEADS = 4
 FILL = 1e-6
 INV_DH = 1.0 / 128.0
+BIG = 1e30
 N_MASKED = 128 * 129 // 2
 ROWS = 64
 QUADS = 8
 GROUP = 4
 
-CHUNK_MASKED = ((64, 0), (64, 32))
-CHUNK_DIAG_A = ((0, 0), (64, 64))
-CHUNK_DIAG_B = ((0, 32), (64, 96))
-CHUNK_LIVE = ((0, 64), (0, 96))
-CHUNKS = (CHUNK_MASKED, CHUNK_DIAG_A, CHUNK_DIAG_B, CHUNK_LIVE)
+LIVE, MASKED, DIAG_A, DIAG_B = 0, 1, 2, 3
+CHUNKS = (((0, 64), (0, 96)), ((64, 0), (64, 32)), ((0, 0), (64, 64)), ((0, 32), (64, 96)))
 
 ER_WIDTH = GROUP * 512 + 256
 
 FLOPS = 2 * 128 * 512 * 128 * 128 + 2 * 4 * 128 * 16384 * 128 + 2 * 128 * 512 * 512
 
 
-def rows_below_diagonal(chunk, quad):
-    p0, q0 = chunk[0]
+def rows_below_diagonal(ci, quad):
+    p0, q0 = CHUNKS[ci][0]
     return min(ROWS, max(0, q0 - p0 + 4 * quad))
+
+
+STAT_COLS = 3 * QUADS + 1
+
+
+def stat_col(ci, quad):
+    return QUADS * (0 if ci == LIVE else ci - 1) + quad
 
 
 def tile_trittentioncube_pb_kernel(tc, a_heads, step2, v_pairs, W_out, b_out, out):
     nc = tc.nc
     v_plane = v_pairs.rearrange("n (p q) f -> n p q f", q=P)
+    scored = [(ci, quad) for ci in (LIVE, DIAG_A, DIAG_B) for quad in range(QUADS) if rows_below_diagonal(ci, quad) > 0]
 
     with ExitStack() as stack:
         keep = stack.enter_context(tc.tile_pool(name="keep", bufs=1))
@@ -56,56 +62,45 @@ def tile_trittentioncube_pb_kernel(tc, a_heads, step2, v_pairs, W_out, b_out, ou
         bias_rows = keep.tile([P, 512], BF16)
         v_codes = keep.tile([P, HEADS, len(CHUNKS), QUADS, P], U32, align_bytes=64)
         v_scales = keep.tile([P, HEADS, len(CHUNKS), QUADS, P], U8, align_bytes=64)
-        part_max = keep.tile([P, P, HEADS], F32)
+        part_max = keep.tile([P, HEADS, STAT_COLS], F32)
+        sums = keep.tile([P, HEADS, STAT_COLS], F32)
         top = keep.tile([P, HEADS], F32)
         neg_m = keep.tile([P, HEADS], F32)
         e_fill = keep.tile([P, HEADS], F32)
-        live01 = keep.tile([P, 32], F32)
-        mask01 = keep.tile([P, 32], F32)
-        diag_e = keep.tile([P, HEADS, 512], F32)
-        diag_sum = keep.tile([P, HEADS], F32)
-        diag_bf = keep.tile([P, HEADS, 512], BF16)
-        sums = keep.tile([P, HEADS, 24], F32)
         total = keep.tile([P, HEADS], F32)
         recip = keep.tile([P, HEADS], F32)
+        bound = keep.tile([P, 32], F32)
+        mask01 = keep.tile([P, 32], F32)
+        diag_s = keep.tile([P, HEADS, 16, 32], F32)
+        diag_e = keep.tile([P, HEADS, 512], F32)
+        diag_bf = keep.tile([P, HEADS, 512], BF16)
         z_bf = keep.tile([P, HEADS * P], BF16)
+
+        nc.vector.memset(bound, -BIG)
+        nc.vector.memset(mask01, 1.0)
+        for t in range(1, 4):
+            for cells, value in ((bound, BIG), (mask01, 0.0)):
+                nc.vector.memset(
+                    cells.rearrange("r (u j h e) -> r u j h e", u=2, j=4, h=2)[:, t // 2, 0:t, :, t % 2], value
+                )
+        nc.vector.memset(part_max, FILL)
+        nc.vector.memset(sums, 0.0)
 
         with tc.tile_pool(name="early", bufs=1) as early, tc.psum_pool(name="ps_early", bufs=1) as ps_early:
             a_rows = early.tile([P, HEADS * P], BF16)
             nc.sync.dma_start(out=a_rows, in_=a_heads.rearrange("p n i -> p (n i)"))
+            w_rows = early.tile([P, 4, 512], BF16)
+            nc.sync.dma_start(out=w_rows, in_=W_out.rearrange("(c o) k -> o c k", o=P))
             s_raw = early.tile([P, P, P], BF16)
             for rc in range(8):
                 r_cols = slice(16 * rc, 16 * rc + 16)
                 nc.sync.dma_start(out=s_raw[:, r_cols, :], in_=step2[r_cols].rearrange("r i q -> i r q"))
-            w_rows = early.tile([P, 4, 512], BF16)
-            nc.sync.dma_start(out=w_rows, in_=W_out.rearrange("(c o) k -> o c k", o=P))
             nc.sync.dma_start(out=bias_rows, in_=b_out.partition_broadcast(P))
 
             a_ps = ps_early.tile([P, HEADS, P], BF16)
             for n in range(HEADS):
                 nc.tensor.transpose(a_ps[:, n, :], a_rows[:, n * P : (n + 1) * P], ident_bf)
             nc.vector.tensor_copy(out=a_t, in_=a_ps)
-
-            for rc in range(8):
-                r_cols = slice(16 * rc, 16 * rc + 16)
-                src = s_raw[:, r_cols, :].rearrange("i r q -> i q r")
-                if rc % 2 == 0:
-                    nc.vector.tensor_copy(out=s2[:, :, r_cols], in_=src)
-                elif rc % 4 == 1:
-                    nc.scalar.copy(out=s2[:, :, r_cols], in_=src)
-                else:
-                    nc.gpsimd.tensor_scalar(
-                        out=s2[:, :, r_cols], in0=src, scalar1=1.0, scalar2=0.0, op0=ALU.mult, op1=ALU.add
-                    )
-
-            nc.vector.memset(part_max[:, 0, :], FILL)
-            for q in range(1, P):
-                s_ps = ps_early.tile([P, HEADS, P], F32, bufs=4)
-                nc.tensor.matmul(out=s_ps[:, :, 0:q], lhsT=s2[:, q, :], rhs=a_t[:, :, 0:q], start=True, stop=True)
-                nc.vector.tensor_reduce(out=part_max[:, q, :], in_=s_ps[:, :, 0:q], axis=AX.X, op=ALU.max)
-            nc.vector.tensor_reduce(out=top, in_=part_max.rearrange("r q n -> r n q"), axis=AX.X, op=ALU.max)
-            nc.vector.tensor_scalar(out=neg_m, in0=top, scalar1=-INV_DH, scalar2=None, op0=ALU.mult)
-            nc.scalar.activation(out=e_fill, in_=neg_m, func=ACT.Exp, bias=FILL * INV_DH, scale=1.0)
 
             w_words = w_rows.bitcast(F32)
             w_grouped = early.tile([P, 2048], BF16, align_bytes=64)
@@ -120,51 +115,105 @@ def tile_trittentioncube_pb_kernel(tc, a_heads, step2, v_pairs, W_out, b_out, ou
                 )
             nc.vector.quantize_mx(out=w_codes.bitcast(FP8X4), scales=w_scales, in_=w_grouped)
 
+            for rc in range(8):
+                r_cols = slice(16 * rc, 16 * rc + 16)
+                src = s_raw[:, r_cols, :].rearrange("i r q -> i q r")
+                if rc % 4 == 0:
+                    nc.gpsimd.tensor_scalar(
+                        out=s2[:, :, r_cols], in0=src, scalar1=1.0, scalar2=0.0, op0=ALU.mult, op1=ALU.add
+                    )
+                elif rc % 4 == 1:
+                    nc.scalar.copy(out=s2[:, :, r_cols], in_=src)
+                else:
+                    nc.vector.tensor_copy(out=s2[:, :, r_cols], in_=src)
+
         stream = stack.enter_context(tc.tile_pool(name="stream", bufs=3))
         e_pool = stack.enter_context(tc.tile_pool(name="e_pool", bufs=2))
-        ps_s = stack.enter_context(tc.psum_pool(name="ps_s", bufs=3))
+        ps_s = stack.enter_context(tc.psum_pool(name="ps_s", bufs=4))
         ps_t = stack.enter_context(tc.psum_pool(name="ps_t", bufs=2))
         ps_z = stack.enter_context(tc.psum_pool(name="ps_z", bufs=2))
-        ps_o = stack.enter_context(tc.psum_pool(name="ps_o", bufs=1))
 
-        live_cells = live01.rearrange("r (u j h e) -> r u j h e", u=2, j=4, h=2)
-        nc.vector.memset(live01, 0.0)
-        for t in range(1, 4):
-            nc.vector.memset(live_cells[:, t // 2, 0:t, :, t % 2], 1.0)
-        nc.vector.tensor_scalar(out=mask01, in0=live01, scalar1=-1.0, scalar2=1.0, op0=ALU.mult, op1=ALU.add)
-        nc.vector.memset(sums, 0.0)
+        v_order = [(n, ci) for n in range(HEADS) for ci in range(len(CHUNKS))]
+        v_raw = {}
+        v_grouped = {}
 
-        for bank in range(4):
-            d_ps = ps_s.tile([P, 512], F32, name="s_ps")
-            d_cells = d_ps.rearrange("r (n s u j h e) -> r n s u j h e", n=HEADS, s=4, u=2, j=4, h=2)
-            for s_in in range(4):
-                s = 4 * bank + s_in
-                for h in range(2):
-                    corner = 64 * h + 4 * s
-                    for t in range(4):
-                        nc.tensor.matmul(
-                            out=d_cells[:, :, s_in, t // 2, :, h, t % 2],
-                            lhsT=s2[:, corner + t, :],
-                            rhs=a_t[:, :, corner : corner + 4],
-                            start=True,
-                            stop=True,
-                        )
-            for n in range(HEADS):
-                nc.scalar.activation(
-                    out=diag_e[:, n, bank * P : (bank + 1) * P],
-                    in_=d_ps[:, n * P : (n + 1) * P],
-                    func=ACT.Exp,
-                    bias=neg_m[:, n : n + 1],
-                    scale=INV_DH,
-                )
-        nc.vector.tensor_tensor(
-            out=diag_e.rearrange("r n (s x) -> r (n s) x", x=32),
-            in0=diag_e.rearrange("r n (s x) -> r (n s) x", x=32),
-            in1=live01.unsqueeze(1).to_broadcast([P, HEADS * 16, 32]),
-            op=ALU.min,
-        )
-        nc.vector.tensor_reduce(out=diag_sum, in_=diag_e, axis=AX.X, op=ALU.add)
-        for n in range(HEADS):
+        def load_v(k):
+            if k < len(v_order):
+                n, ci = v_order[k]
+                v_raw[k] = stream.tile([P, 4 * QUADS, P], BF16, name="v_raw")
+                for h, (p0, q0) in enumerate(CHUNKS[ci]):
+                    nc.sync.dma_start(out=v_raw[k][h:P:2, :, :], in_=v_plane[n, p0 : p0 + ROWS, q0 : q0 + 4 * QUADS, :])
+
+        def regroup_v(k):
+            v_grouped[k] = stream.tile([P, QUADS, P, 4], BF16, align_bytes=64, name="v_grouped")
+            nc.scalar.copy(out=v_grouped[k][:, 0:4], in_=v_raw[k][:, 0:16, :].rearrange("x (j t) f -> x j f t", t=4))
+            nc.gpsimd.tensor_scalar(
+                out=v_grouped[k][:, 4:8], in0=v_raw[k][:, 16:32, :].rearrange("x (j t) f -> x j f t", t=4),
+                scalar1=1.0, scalar2=0.0, op0=ALU.mult, op1=ALU.add,
+            )
+
+        def quantise_v(k):
+            n, ci = v_order[k]
+            nc.vector.quantize_mx(
+                out=v_codes[:, n, ci].rearrange("x j f -> x (j f)").bitcast(FP8X4),
+                scales=v_scales[:, n, ci].rearrange("x j f -> x (j f)"),
+                in_=v_grouped[k].rearrange("x j f t -> x (j f t)"),
+            )
+
+        def step_v(k):
+            load_v(k + 2)
+            if k > 0:
+                quantise_v(k - 1)
+            regroup_v(k)
+
+        def scores(n, ci, quad):
+            rows = rows_below_diagonal(ci, quad)
+            s_ps = ps_s.tile([P, 512], F32)
+            cells = s_ps[:, 0 : 8 * rows].rearrange("r (u p h e) -> r u p h e", u=2, h=2, e=2)
+            for h, (p0, q0) in enumerate(CHUNKS[ci]):
+                for t in range(4):
+                    nc.tensor.matmul(
+                        out=cells[:, t // 2, :, h, t % 2],
+                        lhsT=s2[:, q0 + 4 * quad + t, :],
+                        rhs=a_t[:, n, p0 : p0 + rows],
+                        start=True,
+                        stop=True,
+                    )
+            return s_ps[:, 0 : 8 * rows]
+
+        def maximum_of(n, ci, quad):
+            col = stat_col(ci, quad)
+            nc.vector.tensor_reduce(out=part_max[:, n, col : col + 1], in_=scores(n, ci, quad), axis=AX.X, op=ALU.max)
+
+        def filled_with_e_fill(n, width, name):
+            e_tile = e_pool.tile([P, width], BF16, name=name)
+            used = width // 512 * 512
+            nc.gpsimd.tensor_scalar(
+                out=e_tile[:, 0:used], in0=e_fill[:, n : n + 1].to_broadcast([P, used]),
+                scalar1=1.0, scalar2=0.0, op0=ALU.mult, op1=ALU.add,
+            )
+            return e_tile
+
+        e_const = {}
+        e_diag = {}
+
+        def statistics_of(n):
+            one = slice(n, n + 1)
+            nc.vector.tensor_reduce(out=top[:, one], in_=part_max[:, n, :], axis=AX.X, op=ALU.max)
+            nc.vector.tensor_scalar(out=neg_m[:, one], in0=top[:, one], scalar1=-INV_DH, scalar2=None, op0=ALU.mult)
+            nc.scalar.activation(out=e_fill[:, one], in_=neg_m[:, one], func=ACT.Exp, bias=FILL * INV_DH, scale=1.0)
+            nc.scalar.activation(
+                out=diag_e[:, n, :],
+                in_=diag_s[:, n].rearrange("r s x -> r (s x)"),
+                func=ACT.Exp,
+                bias=neg_m[:, one],
+                scale=INV_DH,
+                accum_out=sums[:, n, STAT_COLS - 1 : STAT_COLS],
+            )
+            e_const[n] = filled_with_e_fill(n, 512, "e_const")
+            e_diag[n] = [filled_with_e_fill(n, ER_WIDTH, "e_diag%d" % half) for half in range(2)]
+
+        def diagonal_blocks_of(n):
             nc.vector.scalar_tensor_tensor(
                 out=diag_bf[:, n, :].rearrange("r (s x) -> r s x", x=32),
                 in0=mask01.unsqueeze(1).to_broadcast([P, 16, 32]),
@@ -174,45 +223,46 @@ def tile_trittentioncube_pb_kernel(tc, a_heads, step2, v_pairs, W_out, b_out, ou
                 op1=ALU.add,
             )
 
-        def load_and_quantise_v(n, ci):
-            raw = stream.tile([P, 4 * QUADS, P], BF16)
-            for h, (p0, q0) in enumerate(CHUNKS[ci]):
-                nc.sync.dma_start(out=raw[h:P:2, :, :], in_=v_plane[n, p0 : p0 + ROWS, q0 : q0 + 4 * QUADS, :])
-            grouped = stream.tile([P, QUADS, P, 4], BF16, align_bytes=64)
-            nc.vector.tensor_copy(
-                out=grouped[:, 0:4].rearrange("x j (c i) t -> x j c t i", i=4),
-                in_=raw[:, 0:16, :].rearrange("x (j t) (c i) -> x j c t i", t=4, i=4),
-            )
-            nc.scalar.copy(out=grouped[:, 4:8], in_=raw[:, 16:32, :].rearrange("x (j t) f -> x j f t", t=4))
-            nc.vector.quantize_mx(
-                out=v_codes[:, n, ci].rearrange("x j f -> x (j f)").bitcast(FP8X4),
-                scales=v_scales[:, n, ci].rearrange("x j f -> x (j f)"),
-                in_=grouped.rearrange("x j f t -> x (j f t)"),
-            )
+        units = [
+            (n, ci, half)
+            for n in range(HEADS)
+            for ci, half in ((LIVE, 0), (LIVE, 1), (MASKED, 0), (DIAG_A, 0), (DIAG_A, 1), (DIAG_B, 0), (DIAG_B, 1))
+        ]
+        per_head = len(units) // HEADS
+        e_rows = {}
+        e_grouped = {}
+        e_codes = {}
+        z_ps = {}
 
-        def scores_and_exp(n, chunk, quad, e_rows, sum_col):
-            rows = rows_below_diagonal(chunk, quad)
-            s_ps = ps_s.tile([P, 512], F32)
-            cells = s_ps[:, 0 : 8 * rows].rearrange("r (u p h e) -> r u p h e", u=2, h=2, e=2)
-            for h, (p0, q0) in enumerate(chunk):
-                for t in range(4):
-                    nc.tensor.matmul(
-                        out=cells[:, t // 2, :, h, t % 2],
-                        lhsT=s2[:, q0 + 4 * quad + t, :],
-                        rhs=a_t[:, n, p0 : p0 + rows],
-                        start=True,
-                        stop=True,
+        def exp_stage(i):
+            n, ci, half = units[i]
+            if ci == MASKED:
+                e_rows[i] = e_const[n]
+                return
+            e_rows[i] = e_pool.tile([P, GROUP * 512], BF16, name="e_live") if ci == LIVE else e_diag[n][half]
+            if ci != LIVE:
+                s0 = rows_below_diagonal(ci, GROUP * half) // 4
+                nc.vector.tensor_copy(
+                    out=e_rows[i][:, 16 * s0 : 16 * s0 + GROUP * 528]
+                    .rearrange("r (g y) -> r g y", y=528)[:, :, 0:512]
+                    .rearrange("r g (u x) -> r g u x", u=2)[:, :, :, 0:16],
+                    in_=diag_bf[:, n, 32 * s0 : 32 * (s0 + GROUP)].rearrange("r (g u x) -> r g u x", g=GROUP, u=2),
+                )
+            for g in range(GROUP):
+                quad = GROUP * half + g
+                rows = rows_below_diagonal(ci, quad)
+                if rows > 0:
+                    col = stat_col(ci, quad)
+                    nc.scalar.activation(
+                        out=e_rows[i][:, 512 * g : 512 * (g + 1)].rearrange("r (u x) -> r u x", u=2)[:, :, 0 : 4 * rows],
+                        in_=scores(n, ci, quad).rearrange("r (u x) -> r u x", u=2),
+                        func=ACT.Exp,
+                        bias=neg_m[:, n : n + 1],
+                        scale=INV_DH,
+                        accum_out=sums[:, n, col : col + 1],
                     )
-            nc.scalar.activation(
-                out=e_rows[:, :, 0 : 4 * rows],
-                in_=s_ps[:, 0 : 8 * rows].rearrange("r (u x) -> r u x", u=2),
-                func=ACT.Exp,
-                bias=neg_m[:, n : n + 1],
-                scale=INV_DH,
-                accum_out=sums[:, n, sum_col : sum_col + 1],
-            )
 
-        def transpose_and_quantise(e_words, passes):
+        def transpose_rows(e_words, passes):
             grouped = e_pool.tile([P, GROUP * 512], BF16, align_bytes=64, name="e_grouped")
             grouped_words = grouped.bitcast(F32).rearrange("x (g r u) -> x g r u", g=GROUP, u=2)
             for first in range(0, passes, 2):
@@ -222,11 +272,14 @@ def tile_trittentioncube_pb_kernel(tc, a_heads, step2, v_pairs, W_out, b_out, ou
                     for u in range(2):
                         start_word = 256 * (first + g) + P * u
                         nc.tensor.transpose(t_ps[:, g, u, :], e_words[:, start_word : start_word + P], ident_f32)
-                copy_out = nc.scalar.copy if first % 4 == 0 else nc.vector.tensor_copy
+                copy_out = nc.vector.tensor_copy if first == 0 else nc.scalar.copy
                 copy_out(
                     out=grouped_words[:, first : first + pair],
                     in_=t_ps[:, 0:pair].rearrange("x g u r -> x g r u"),
                 )
+            return grouped
+
+        def quantise_rows(grouped, passes):
             codes = e_pool.tile([P, GROUP * P], U32, align_bytes=64, name="e_codes")
             scales = e_pool.tile([P, GROUP * P], U8, align_bytes=64, name="e_scales")
             nc.vector.quantize_mx(
@@ -236,90 +289,106 @@ def tile_trittentioncube_pb_kernel(tc, a_heads, step2, v_pairs, W_out, b_out, ou
             )
             return codes, scales
 
-        def multiply(z_ps, n, codes, scales, g, ci, quad):
-            nc.tensor.matmul_mx(
-                out=z_ps,
-                lhsT=codes[:, g * P : (g + 1) * P].bitcast(FP8X4),
-                lhsT_scale=scales[:, g * P : (g + 1) * P],
-                rhs=v_codes[:, n, ci, quad, :].bitcast(FP8X4),
-                rhs_scale=v_scales[:, n, ci, quad, :],
-                start=(ci == 0 and quad == 0),
-                stop=(ci == len(CHUNKS) - 1 and quad == QUADS - 1),
-            )
+        def passes_of(i):
+            return 1 if units[i][1] == MASKED else GROUP
 
-        for n in range(HEADS):
-            for ci in range(len(CHUNKS)):
-                load_and_quantise_v(n, ci)
-
-            z_ps = ps_z.tile([P, P], F32)
-
-            e_const = e_pool.tile([P, 512], BF16)
-            nc.gpsimd.tensor_scalar(
-                out=e_const, in0=e_fill[:, n : n + 1].to_broadcast([P, 512]),
-                scalar1=1.0, scalar2=0.0, op0=ALU.mult, op1=ALU.add,
-            )
-            e_diag = []
-            for half in range(2):
-                e_tile = e_pool.tile([P, ER_WIDTH], BF16, name="e_diag%d" % half)
-                nc.gpsimd.tensor_scalar(
-                    out=e_tile[:, 0 : GROUP * 512], in0=e_fill[:, n : n + 1].to_broadcast([P, GROUP * 512]),
-                    scalar1=1.0, scalar2=0.0, op0=ALU.mult, op1=ALU.add,
+        def multiply_stage(i):
+            n, ci, half = units[i]
+            codes, scales = e_codes[i]
+            if i % per_head == 0:
+                z_ps[n] = ps_z.tile([P, P], F32, name="z_ps")
+            for quad in range(QUADS) if ci == MASKED else range(GROUP * half, GROUP * (half + 1)):
+                g = 0 if ci == MASKED else quad - GROUP * half
+                nc.tensor.matmul_mx(
+                    out=z_ps[n],
+                    lhsT=codes[:, g * P : (g + 1) * P].bitcast(FP8X4),
+                    lhsT_scale=scales[:, g * P : (g + 1) * P],
+                    rhs=v_codes[:, n, ci, quad, :].bitcast(FP8X4),
+                    rhs_scale=v_scales[:, n, ci, quad, :],
+                    start=(ci == 0 and quad == 0),
+                    stop=(ci == len(CHUNKS) - 1 and quad == QUADS - 1),
                 )
-                e_diag.append(e_tile)
+            if i % per_head == per_head - 1:
+                one = slice(n, n + 1)
+                nc.vector.tensor_reduce(out=total[:, one], in_=sums[:, n, :], axis=AX.X, op=ALU.add)
+                nc.vector.scalar_tensor_tensor(
+                    out=total[:, one], in0=e_fill[:, one], scalar=float(N_MASKED), in1=total[:, one],
+                    op0=ALU.mult, op1=ALU.add,
+                )
+                nc.vector.reciprocal(out=recip[:, one], in_=total[:, one])
+                nc.scalar.activation(out=z_bf[:, n * P : (n + 1) * P], in_=z_ps[n], func=ACT.Copy, scale=recip[:, one])
 
-            codes, scales = transpose_and_quantise(e_const.bitcast(F32), 1)
-            for quad in range(QUADS):
-                multiply(z_ps, n, codes, scales, 0, 0, quad)
+        with tc.manual_schedule():
+            load_v(0)
+            load_v(1)
 
-            for ci in (1, 2, 3):
-                chunk = CHUNKS[ci]
-                for half in range(2):
-                    on_diagonal = ci < 3
-                    if on_diagonal:
-                        e_tile = e_diag[half]
-                    else:
-                        e_tile = e_pool.tile([P, GROUP * 512], BF16, name="e_live")
-                    for g in range(GROUP):
-                        quad = GROUP * half + g
-                        if rows_below_diagonal(chunk, quad) > 0:
-                            scores_and_exp(
-                                n, chunk, quad,
-                                e_tile[:, 512 * g : 512 * (g + 1)].rearrange("r (u x) -> r u x", u=2),
-                                QUADS * (ci - 1) + quad,
+            for bank in range(4):
+                d_ps = ps_s.tile([P, 512], F32, name="s_ps")
+                d_cells = d_ps.rearrange("r (n s u j h e) -> r n s u j h e", n=HEADS, s=4, u=2, j=4, h=2)
+                for s_in in range(4):
+                    for h in range(2):
+                        corner = 64 * h + 4 * (4 * bank + s_in)
+                        for t in range(4):
+                            nc.tensor.matmul(
+                                out=d_cells[:, :, s_in, t // 2, :, h, t % 2],
+                                lhsT=s2[:, corner + t, :],
+                                rhs=a_t[:, :, corner : corner + 4],
+                                start=True,
+                                stop=True,
                             )
-                    if on_diagonal:
-                        s0 = rows_below_diagonal(chunk, GROUP * half) // 4
-                        nc.vector.tensor_copy(
-                            out=e_tile[:, 16 * s0 : 16 * s0 + GROUP * 528]
-                            .rearrange("r (g y) -> r g y", y=528)[:, :, 0:512]
-                            .rearrange("r g (u x) -> r g u x", u=2)[:, :, :, 0:16],
-                            in_=diag_bf[:, n, 32 * s0 : 32 * (s0 + GROUP)].rearrange("r (g u x) -> r g u x", g=GROUP, u=2),
-                        )
-                    codes, scales = transpose_and_quantise(e_tile.bitcast(F32), GROUP)
-                    for g in range(GROUP):
-                        multiply(z_ps, n, codes, scales, g, ci, GROUP * half + g)
-
-            one = slice(n, n + 1)
-            nc.vector.tensor_reduce(out=total[:, one], in_=sums[:, n, :], axis=AX.X, op=ALU.add)
-            nc.vector.tensor_tensor(out=total[:, one], in0=total[:, one], in1=diag_sum[:, one], op=ALU.add)
-            nc.vector.scalar_tensor_tensor(
-                out=total[:, one], in0=e_fill[:, one], scalar=float(N_MASKED), in1=total[:, one],
-                op0=ALU.mult, op1=ALU.add,
+                nc.vector.tensor_tensor(
+                    out=diag_s[:, :, 4 * bank : 4 * bank + 4, :],
+                    in0=d_ps.rearrange("r (n s x) -> r n s x", n=HEADS, s=4),
+                    in1=bound.unsqueeze(1).unsqueeze(1).to_broadcast([P, HEADS, 4, 32]),
+                    op=ALU.min,
+                )
+            nc.vector.tensor_reduce(
+                out=part_max[:, :, STAT_COLS - 1 : STAT_COLS],
+                in_=diag_s.rearrange("r n s x -> r n (s x)"),
+                axis=AX.X,
+                op=ALU.max,
             )
-            nc.vector.reciprocal(out=recip[:, one], in_=total[:, one])
-            nc.scalar.activation(out=z_bf[:, n * P : (n + 1) * P], in_=z_ps, func=ACT.Copy, scale=recip[:, one])
 
-        z_codes, z_scales = transpose_and_quantise(z_bf.bitcast(F32), 1)
-        o_ps = ps_o.tile([P, 512], F32)
-        nc.tensor.matmul_mx(
-            out=o_ps,
-            lhsT=z_codes[:, 0:P].bitcast(FP8X4),
-            lhsT_scale=z_scales[:, 0:P],
-            rhs=w_codes.bitcast(FP8X4),
-            rhs_scale=w_scales,
-            start=True,
-            stop=True,
-        )
-        o_sb = keep.tile([P, 512], F32)
-        nc.vector.tensor_tensor(out=o_sb, in0=o_ps, in1=bias_rows, op=ALU.add)
-        nc.sync.dma_start(out=out, in_=o_sb)
+            for k, (ci, quad) in enumerate(scored):
+                maximum_of(0, ci, quad)
+                if k % 6 == 0:
+                    step_v(k // 6)
+            statistics_of(0)
+            diagonal_blocks_of(0)
+
+            for i in range(len(units) + 3):
+                if i < len(units):
+                    exp_stage(i)
+                if 0 <= i - 1 < len(units):
+                    e_grouped[i - 1] = transpose_rows(e_rows[i - 1].bitcast(F32), passes_of(i - 1))
+                if 0 <= i - 2 < len(units):
+                    e_codes[i - 2] = quantise_rows(e_grouped[i - 2], passes_of(i - 2))
+                if i < len(units) - per_head:
+                    n, k = i // per_head, i % per_head
+                    for ci, quad in scored[4 * k : 4 * k + 4]:
+                        maximum_of(n + 1, ci, quad)
+                    if k == per_head - 1:
+                        statistics_of(n + 1)
+                    if k % 2 == 0:
+                        step_v(len(CHUNKS) * (n + 1) + k // 2)
+                if i == len(units) - per_head:
+                    quantise_v(len(v_order) - 1)
+                if 0 <= i - 3:
+                    multiply_stage(i - 3)
+                if i < len(units) - per_head and i % per_head == per_head - 1:
+                    diagonal_blocks_of(i // per_head + 1)
+
+            z_codes, z_scales = quantise_rows(transpose_rows(z_bf.bitcast(F32), 1), 1)
+            o_ps = ps_s.tile([P, 512], F32, name="s_ps")
+            nc.tensor.matmul_mx(
+                out=o_ps,
+                lhsT=z_codes[:, 0:P].bitcast(FP8X4),
+                lhsT_scale=z_scales[:, 0:P],
+                rhs=w_codes.bitcast(FP8X4),
+                rhs_scale=w_scales,
+                start=True,
+                stop=True,
+            )
+            o_sb = keep.tile([P, 512], F32)
+            nc.vector.tensor_tensor(out=o_sb, in0=o_ps, in1=bias_rows, op=ALU.add)
+            nc.sync.dma_start(out=out, in_=o_sb)

@@ -72,8 +72,7 @@ def tile_trittentioncube_pb_kernel(tc, a_heads, step2, v_pairs, W_out, b_out, ou
         bound = keep.tile([P, 32], F32)
         mask01 = keep.tile([P, 32], F32)
         diag_s = keep.tile([P, HEADS, 16, 32], F32)
-        diag_e = keep.tile([P, HEADS, 512], F32)
-        diag_bf = keep.tile([P, HEADS, 512], BF16)
+        s_kept = keep.tile([P, 8 * sum(rows_below_diagonal(ci, quad) for ci, quad in scored)], F32)
         z_bf = keep.tile([P, HEADS * P], BF16)
 
         nc.vector.memset(bound, -BIG)
@@ -127,7 +126,7 @@ def tile_trittentioncube_pb_kernel(tc, a_heads, step2, v_pairs, W_out, b_out, ou
                 else:
                     nc.vector.tensor_copy(out=s2[:, :, r_cols], in_=src)
 
-        stream = stack.enter_context(tc.tile_pool(name="stream", bufs=3))
+        stream = stack.enter_context(tc.tile_pool(name="stream", bufs=2))
         e_pool = stack.enter_context(tc.tile_pool(name="e_pool", bufs=2))
         ps_s = stack.enter_context(tc.psum_pool(name="ps_s", bufs=4))
         ps_t = stack.enter_context(tc.psum_pool(name="ps_t", bufs=2))
@@ -161,7 +160,7 @@ def tile_trittentioncube_pb_kernel(tc, a_heads, step2, v_pairs, W_out, b_out, ou
             )
 
         def step_v(k):
-            load_v(k + 2)
+            load_v(k + 1)
             if k > 0:
                 quantise_v(k - 1)
             regroup_v(k)
@@ -181,12 +180,25 @@ def tile_trittentioncube_pb_kernel(tc, a_heads, step2, v_pairs, W_out, b_out, ou
                     )
             return s_ps[:, 0 : 8 * rows]
 
-        def maximum_of(n, ci, quad):
+        kept_cols = {}
+        for ci, quad in scored:
+            first = 8 * sum(rows_below_diagonal(*earlier) for earlier in kept_cols)
+            kept_cols[(ci, quad)] = slice(first, first + 8 * rows_below_diagonal(ci, quad))
+
+        def scores_and_maximum(n, ci, quad):
             col = stat_col(ci, quad)
-            nc.vector.tensor_reduce(out=part_max[:, n, col : col + 1], in_=scores(n, ci, quad), axis=AX.X, op=ALU.max)
+            nc.vector.tensor_scalar(
+                out=s_kept[:, kept_cols[(ci, quad)]],
+                in0=scores(n, ci, quad),
+                scalar1=1.0,
+                scalar2=None,
+                op0=ALU.mult,
+                op1=ALU.max,
+                accum_out=part_max[:, n, col : col + 1],
+            )
 
         def filled_with_e_fill(n, width, name):
-            e_tile = e_pool.tile([P, width], BF16, name=name)
+            e_tile = e_pool.tile([P, width], BF16, name=name, bufs=1)
             used = width // 512 * 512
             nc.gpsimd.tensor_scalar(
                 out=e_tile[:, 0:used], in0=e_fill[:, n : n + 1].to_broadcast([P, used]),
@@ -196,14 +208,17 @@ def tile_trittentioncube_pb_kernel(tc, a_heads, step2, v_pairs, W_out, b_out, ou
 
         e_const = {}
         e_diag = {}
+        diag_e = {}
+        diag_bf = {}
 
         def statistics_of(n):
             one = slice(n, n + 1)
             nc.vector.tensor_reduce(out=top[:, one], in_=part_max[:, n, :], axis=AX.X, op=ALU.max)
             nc.vector.tensor_scalar(out=neg_m[:, one], in0=top[:, one], scalar1=-INV_DH, scalar2=None, op0=ALU.mult)
             nc.scalar.activation(out=e_fill[:, one], in_=neg_m[:, one], func=ACT.Exp, bias=FILL * INV_DH, scale=1.0)
+            diag_e[n] = e_pool.tile([P, 512], F32, name="diag_e")
             nc.scalar.activation(
-                out=diag_e[:, n, :],
+                out=diag_e[n],
                 in_=diag_s[:, n].rearrange("r s x -> r (s x)"),
                 func=ACT.Exp,
                 bias=neg_m[:, one],
@@ -214,11 +229,12 @@ def tile_trittentioncube_pb_kernel(tc, a_heads, step2, v_pairs, W_out, b_out, ou
             e_diag[n] = [filled_with_e_fill(n, ER_WIDTH, "e_diag%d" % half) for half in range(2)]
 
         def diagonal_blocks_of(n):
+            diag_bf[n] = e_pool.tile([P, 512], BF16, name="diag_bf")
             nc.vector.scalar_tensor_tensor(
-                out=diag_bf[:, n, :].rearrange("r (s x) -> r s x", x=32),
+                out=diag_bf[n].rearrange("r (s x) -> r s x", x=32),
                 in0=mask01.unsqueeze(1).to_broadcast([P, 16, 32]),
                 scalar=e_fill[:, n : n + 1],
-                in1=diag_e[:, n, :].rearrange("r (s x) -> r s x", x=32),
+                in1=diag_e[n].rearrange("r (s x) -> r s x", x=32),
                 op0=ALU.mult,
                 op1=ALU.add,
             )
@@ -246,7 +262,7 @@ def tile_trittentioncube_pb_kernel(tc, a_heads, step2, v_pairs, W_out, b_out, ou
                     out=e_rows[i][:, 16 * s0 : 16 * s0 + GROUP * 528]
                     .rearrange("r (g y) -> r g y", y=528)[:, :, 0:512]
                     .rearrange("r g (u x) -> r g u x", u=2)[:, :, :, 0:16],
-                    in_=diag_bf[:, n, 32 * s0 : 32 * (s0 + GROUP)].rearrange("r (g u x) -> r g u x", g=GROUP, u=2),
+                    in_=diag_bf[n][:, 32 * s0 : 32 * (s0 + GROUP)].rearrange("r (g u x) -> r g u x", g=GROUP, u=2),
                 )
             for g in range(GROUP):
                 quad = GROUP * half + g
@@ -255,7 +271,7 @@ def tile_trittentioncube_pb_kernel(tc, a_heads, step2, v_pairs, W_out, b_out, ou
                     col = stat_col(ci, quad)
                     nc.scalar.activation(
                         out=e_rows[i][:, 512 * g : 512 * (g + 1)].rearrange("r (u x) -> r u x", u=2)[:, :, 0 : 4 * rows],
-                        in_=scores(n, ci, quad).rearrange("r (u x) -> r u x", u=2),
+                        in_=s_kept[:, kept_cols[(ci, quad)]].rearrange("r (u x) -> r u x", u=2),
                         func=ACT.Exp,
                         bias=neg_m[:, n : n + 1],
                         scale=INV_DH,
@@ -320,7 +336,6 @@ def tile_trittentioncube_pb_kernel(tc, a_heads, step2, v_pairs, W_out, b_out, ou
 
         with tc.manual_schedule():
             load_v(0)
-            load_v(1)
 
             for bank in range(4):
                 d_ps = ps_s.tile([P, 512], F32, name="s_ps")
@@ -350,7 +365,7 @@ def tile_trittentioncube_pb_kernel(tc, a_heads, step2, v_pairs, W_out, b_out, ou
             )
 
             for k, (ci, quad) in enumerate(scored):
-                maximum_of(0, ci, quad)
+                scores_and_maximum(0, ci, quad)
                 if k % 6 == 0:
                     step_v(k // 6)
             statistics_of(0)
@@ -364,13 +379,15 @@ def tile_trittentioncube_pb_kernel(tc, a_heads, step2, v_pairs, W_out, b_out, ou
                 if 0 <= i - 2 < len(units):
                     e_codes[i - 2] = quantise_rows(e_grouped[i - 2], passes_of(i - 2))
                 if i < len(units) - per_head:
-                    n, k = i // per_head, i % per_head
-                    for ci, quad in scored[4 * k : 4 * k + 4]:
-                        maximum_of(n + 1, ci, quad)
-                    if k == per_head - 1:
-                        statistics_of(n + 1)
+                    n, ci, half = units[i]
+                    k = i % per_head
+                    for quad in range(GROUP * half, GROUP * (half + 1)):
+                        if (ci, quad) in kept_cols:
+                            scores_and_maximum(n + 1, ci, quad)
                     if k % 2 == 0:
                         step_v(len(CHUNKS) * (n + 1) + k // 2)
+                    if k == per_head - 1:
+                        statistics_of(n + 1)
                 if i == len(units) - per_head:
                     quantise_v(len(v_order) - 1)
                 if 0 <= i - 3:

@@ -17,15 +17,14 @@ HEADS = 4
 FILL = 1e-6
 INV_DH = 1.0 / 128.0
 BIG = 1e30
-N_MASKED = 128 * 129 // 2
 ROWS = 64
 QUADS = 8
 GROUP = 4
+PASS = 512
 
-LIVE, MASKED, DIAG_A, DIAG_B = 0, 1, 2, 3
-CHUNKS = (((0, 64), (0, 96)), ((64, 0), (64, 32)), ((0, 0), (64, 64)), ((0, 32), (64, 96)))
-
-ER_WIDTH = GROUP * 512 + 256
+LIVE, DIAG_A, DIAG_B, MASKED = 0, 1, 2, 3
+CHUNKS = (((0, 64), (0, 96)), ((0, 0), (64, 64)), ((0, 32), (64, 96)), ((64, 0), (64, 32)))
+V_ON_VECTOR = 6
 
 FLOPS = 2 * 128 * 512 * 128 * 128 + 2 * 4 * 128 * 16384 * 128 + 2 * 128 * 512 * 512
 
@@ -35,17 +34,11 @@ def rows_below_diagonal(ci, quad):
     return min(ROWS, max(0, q0 - p0 + 4 * quad))
 
 
-STAT_COLS = 3 * QUADS + 1
-
-
-def stat_col(ci, quad):
-    return QUADS * (0 if ci == LIVE else ci - 1) + quad
-
-
 def tile_trittentioncube_pb_kernel(tc, a_heads, step2, v_pairs, W_out, b_out, out):
     nc = tc.nc
     v_plane = v_pairs.rearrange("n (p q) f -> n p q f", q=P)
-    scored = [(ci, quad) for ci in (LIVE, DIAG_A, DIAG_B) for quad in range(QUADS) if rows_below_diagonal(ci, quad) > 0]
+    kept_passes = 3 * QUADS
+    diag_col = kept_passes
 
     with ExitStack() as stack:
         keep = stack.enter_context(tc.tile_pool(name="keep", bufs=1))
@@ -62,28 +55,29 @@ def tile_trittentioncube_pb_kernel(tc, a_heads, step2, v_pairs, W_out, b_out, ou
         bias_rows = keep.tile([P, 512], BF16)
         v_codes = keep.tile([P, HEADS, len(CHUNKS), QUADS, P], U32, align_bytes=64)
         v_scales = keep.tile([P, HEADS, len(CHUNKS), QUADS, P], U8, align_bytes=64)
-        part_max = keep.tile([P, HEADS, STAT_COLS], F32)
-        sums = keep.tile([P, HEADS, STAT_COLS], F32)
+        s_kept = keep.tile([P, kept_passes * PASS + 256], F32)
+        part_max = keep.tile([P, HEADS, kept_passes + 1], F32)
+        sums = keep.tile([P, HEADS, 7], F32)
         top = keep.tile([P, HEADS], F32)
         neg_m = keep.tile([P, HEADS], F32)
-        e_fill = keep.tile([P, HEADS], F32)
         total = keep.tile([P, HEADS], F32)
         recip = keep.tile([P, HEADS], F32)
-        bound = keep.tile([P, 32], F32)
-        mask01 = keep.tile([P, 32], F32)
+        fill_col = keep.tile([P, 1], F32)
+        ceiling = keep.tile([P, 32], F32)
+        floor = keep.tile([P, 32], F32)
         diag_s = keep.tile([P, HEADS, 16, 32], F32)
-        s_kept = keep.tile([P, 8 * sum(rows_below_diagonal(ci, quad) for ci, quad in scored)], F32)
         z_bf = keep.tile([P, HEADS * P], BF16)
 
-        nc.vector.memset(bound, -BIG)
-        nc.vector.memset(mask01, 1.0)
+        nc.gpsimd.memset(s_kept[:, QUADS * PASS : kept_passes * PASS], FILL)
+        nc.vector.memset(fill_col, FILL)
+        nc.vector.memset(part_max, FILL)
+        nc.vector.memset(ceiling, -BIG)
+        nc.vector.memset(floor, FILL)
         for t in range(1, 4):
-            for cells, value in ((bound, BIG), (mask01, 0.0)):
+            for cells, value in ((ceiling, BIG), (floor, -BIG)):
                 nc.vector.memset(
                     cells.rearrange("r (u j h e) -> r u j h e", u=2, j=4, h=2)[:, t // 2, 0:t, :, t % 2], value
                 )
-        nc.vector.memset(part_max, FILL)
-        nc.vector.memset(sums, 0.0)
 
         with tc.tile_pool(name="early", bufs=1) as early, tc.psum_pool(name="ps_early", bufs=1) as ps_early:
             a_rows = early.tile([P, HEADS * P], BF16)
@@ -117,11 +111,7 @@ def tile_trittentioncube_pb_kernel(tc, a_heads, step2, v_pairs, W_out, b_out, ou
             for rc in range(8):
                 r_cols = slice(16 * rc, 16 * rc + 16)
                 src = s_raw[:, r_cols, :].rearrange("i r q -> i q r")
-                if rc % 4 == 0:
-                    nc.gpsimd.tensor_scalar(
-                        out=s2[:, :, r_cols], in0=src, scalar1=1.0, scalar2=0.0, op0=ALU.mult, op1=ALU.add
-                    )
-                elif rc % 4 == 1:
+                if rc % 2 == 0 and rc < 6:
                     nc.scalar.copy(out=s2[:, :, r_cols], in_=src)
                 else:
                     nc.vector.tensor_copy(out=s2[:, :, r_cols], in_=src)
@@ -145,10 +135,13 @@ def tile_trittentioncube_pb_kernel(tc, a_heads, step2, v_pairs, W_out, b_out, ou
 
         def regroup_v(k):
             v_grouped[k] = stream.tile([P, QUADS, P, 4], BF16, align_bytes=64, name="v_grouped")
-            nc.scalar.copy(out=v_grouped[k][:, 0:4], in_=v_raw[k][:, 0:16, :].rearrange("x (j t) f -> x j f t", t=4))
-            nc.gpsimd.tensor_scalar(
-                out=v_grouped[k][:, 4:8], in0=v_raw[k][:, 16:32, :].rearrange("x (j t) f -> x j f t", t=4),
-                scalar1=1.0, scalar2=0.0, op0=ALU.mult, op1=ALU.add,
+            cut = V_ON_VECTOR
+            nc.vector.tensor_copy(
+                out=v_grouped[k][:, 0:cut].rearrange("x j (c i) t -> x j c t i", i=4),
+                in_=v_raw[k][:, 0 : 4 * cut, :].rearrange("x (j t) (c i) -> x j c t i", t=4, i=4),
+            )
+            nc.scalar.copy(
+                out=v_grouped[k][:, cut:QUADS], in_=v_raw[k][:, 4 * cut : 4 * QUADS, :].rearrange("x (j t) f -> x j f t", t=4)
             )
 
         def quantise_v(k):
@@ -165,84 +158,50 @@ def tile_trittentioncube_pb_kernel(tc, a_heads, step2, v_pairs, W_out, b_out, ou
                 quantise_v(k - 1)
             regroup_v(k)
 
-        def scores(n, ci, quad):
-            rows = rows_below_diagonal(ci, quad)
-            s_ps = ps_s.tile([P, 512], F32)
-            cells = s_ps[:, 0 : 8 * rows].rearrange("r (u p h e) -> r u p h e", u=2, h=2, e=2)
-            for h, (p0, q0) in enumerate(CHUNKS[ci]):
-                for t in range(4):
-                    nc.tensor.matmul(
-                        out=cells[:, t // 2, :, h, t % 2],
-                        lhsT=s2[:, q0 + 4 * quad + t, :],
-                        rhs=a_t[:, n, p0 : p0 + rows],
-                        start=True,
-                        stop=True,
+        def scores_and_maximum(n, ci, half):
+            for quad in range(GROUP * half, GROUP * (half + 1)):
+                rows = rows_below_diagonal(ci, quad)
+                if rows > 0:
+                    s_ps = ps_s.tile([P, PASS], F32)
+                    cells = s_ps[:, 0 : 8 * rows].rearrange("r (u p h e) -> r u p h e", u=2, h=2, e=2)
+                    for h, (p0, q0) in enumerate(CHUNKS[ci]):
+                        for t in range(4):
+                            nc.tensor.matmul(
+                                out=cells[:, t // 2, :, h, t % 2],
+                                lhsT=s2[:, q0 + 4 * quad + t, :],
+                                rhs=a_t[:, n, p0 : p0 + rows],
+                                start=True,
+                                stop=True,
+                            )
+                    kept = QUADS * ci + quad
+                    nc.vector.tensor_scalar(
+                        out=s_kept[:, kept * PASS : (kept + 1) * PASS].rearrange("r (u x) -> r u x", u=2)[:, :, 0 : 4 * rows],
+                        in0=s_ps[:, 0 : 8 * rows].rearrange("r (u x) -> r u x", u=2),
+                        scalar1=1.0,
+                        scalar2=None,
+                        op0=ALU.mult,
+                        op1=ALU.max,
+                        accum_out=part_max[:, n, kept : kept + 1],
                     )
-            return s_ps[:, 0 : 8 * rows]
+            if ci != LIVE:
+                s0 = rows_below_diagonal(ci, GROUP * half) // 4
+                first = QUADS * PASS + (PASS + 16) * s0
+                nc.vector.tensor_copy(
+                    out=s_kept[:, first : first + GROUP * (PASS + 16)]
+                    .rearrange("r (g y) -> r g y", g=GROUP)[:, :, 0:PASS]
+                    .rearrange("r g (u x) -> r g u x", u=2)[:, :, :, 0:16],
+                    in_=diag_s[:, n, s0 : s0 + GROUP, :].rearrange("r g (u x) -> r g u x", u=2),
+                )
 
-        kept_cols = {}
-        for ci, quad in scored:
-            first = 8 * sum(rows_below_diagonal(*earlier) for earlier in kept_cols)
-            kept_cols[(ci, quad)] = slice(first, first + 8 * rows_below_diagonal(ci, quad))
-
-        def scores_and_maximum(n, ci, quad):
-            col = stat_col(ci, quad)
-            nc.vector.tensor_scalar(
-                out=s_kept[:, kept_cols[(ci, quad)]],
-                in0=scores(n, ci, quad),
-                scalar1=1.0,
-                scalar2=None,
-                op0=ALU.mult,
-                op1=ALU.max,
-                accum_out=part_max[:, n, col : col + 1],
-            )
-
-        def filled_with_e_fill(n, width, name):
-            e_tile = e_pool.tile([P, width], BF16, name=name, bufs=1)
-            used = width // 512 * 512
-            nc.gpsimd.tensor_scalar(
-                out=e_tile[:, 0:used], in0=e_fill[:, n : n + 1].to_broadcast([P, used]),
-                scalar1=1.0, scalar2=0.0, op0=ALU.mult, op1=ALU.add,
-            )
-            return e_tile
-
-        e_const = {}
-        e_diag = {}
-        diag_e = {}
-        diag_bf = {}
-
-        def statistics_of(n):
+        def maximum_of(n):
             one = slice(n, n + 1)
             nc.vector.tensor_reduce(out=top[:, one], in_=part_max[:, n, :], axis=AX.X, op=ALU.max)
             nc.vector.tensor_scalar(out=neg_m[:, one], in0=top[:, one], scalar1=-INV_DH, scalar2=None, op0=ALU.mult)
-            nc.scalar.activation(out=e_fill[:, one], in_=neg_m[:, one], func=ACT.Exp, bias=FILL * INV_DH, scale=1.0)
-            diag_e[n] = e_pool.tile([P, 512], F32, name="diag_e")
-            nc.scalar.activation(
-                out=diag_e[n],
-                in_=diag_s[:, n].rearrange("r s x -> r (s x)"),
-                func=ACT.Exp,
-                bias=neg_m[:, one],
-                scale=INV_DH,
-                accum_out=sums[:, n, STAT_COLS - 1 : STAT_COLS],
-            )
-            e_const[n] = filled_with_e_fill(n, 512, "e_const")
-            e_diag[n] = [filled_with_e_fill(n, ER_WIDTH, "e_diag%d" % half) for half in range(2)]
-
-        def diagonal_blocks_of(n):
-            diag_bf[n] = e_pool.tile([P, 512], BF16, name="diag_bf")
-            nc.vector.scalar_tensor_tensor(
-                out=diag_bf[n].rearrange("r (s x) -> r s x", x=32),
-                in0=mask01.unsqueeze(1).to_broadcast([P, 16, 32]),
-                scalar=e_fill[:, n : n + 1],
-                in1=diag_e[n].rearrange("r (s x) -> r s x", x=32),
-                op0=ALU.mult,
-                op1=ALU.add,
-            )
 
         units = [
             (n, ci, half)
             for n in range(HEADS)
-            for ci, half in ((LIVE, 0), (LIVE, 1), (MASKED, 0), (DIAG_A, 0), (DIAG_A, 1), (DIAG_B, 0), (DIAG_B, 1))
+            for ci, half in ((LIVE, 0), (LIVE, 1), (DIAG_A, 0), (DIAG_A, 1), (DIAG_B, 0), (DIAG_B, 1), (MASKED, 0))
         ]
         per_head = len(units) // HEADS
         e_rows = {}
@@ -250,36 +209,25 @@ def tile_trittentioncube_pb_kernel(tc, a_heads, step2, v_pairs, W_out, b_out, ou
         e_codes = {}
         z_ps = {}
 
+        def passes_of(i):
+            return 1 if units[i][1] == MASKED else GROUP
+
         def exp_stage(i):
             n, ci, half = units[i]
-            if ci == MASKED:
-                e_rows[i] = e_const[n]
-                return
-            e_rows[i] = e_pool.tile([P, GROUP * 512], BF16, name="e_live") if ci == LIVE else e_diag[n][half]
-            if ci != LIVE:
-                s0 = rows_below_diagonal(ci, GROUP * half) // 4
-                nc.vector.tensor_copy(
-                    out=e_rows[i][:, 16 * s0 : 16 * s0 + GROUP * 528]
-                    .rearrange("r (g y) -> r g y", y=528)[:, :, 0:512]
-                    .rearrange("r g (u x) -> r g u x", u=2)[:, :, :, 0:16],
-                    in_=diag_bf[n][:, 32 * s0 : 32 * (s0 + GROUP)].rearrange("r (g u x) -> r g u x", g=GROUP, u=2),
-                )
-            for g in range(GROUP):
-                quad = GROUP * half + g
-                rows = rows_below_diagonal(ci, quad)
-                if rows > 0:
-                    col = stat_col(ci, quad)
-                    nc.scalar.activation(
-                        out=e_rows[i][:, 512 * g : 512 * (g + 1)].rearrange("r (u x) -> r u x", u=2)[:, :, 0 : 4 * rows],
-                        in_=s_kept[:, kept_cols[(ci, quad)]].rearrange("r (u x) -> r u x", u=2),
-                        func=ACT.Exp,
-                        bias=neg_m[:, n : n + 1],
-                        scale=INV_DH,
-                        accum_out=sums[:, n, col : col + 1],
-                    )
+            width = passes_of(i) * PASS
+            first = (QUADS * ci + GROUP * half) * PASS
+            e_rows[i] = e_pool.tile([P, GROUP * PASS], BF16, name="e_rows")
+            nc.scalar.activation(
+                out=e_rows[i][:, 0:width],
+                in_=fill_col.to_broadcast([P, width]) if ci == MASKED else s_kept[:, first : first + width],
+                func=ACT.Exp,
+                bias=neg_m[:, n : n + 1],
+                scale=INV_DH,
+                accum_out=sums[:, n, i % per_head : i % per_head + 1],
+            )
 
         def transpose_rows(e_words, passes):
-            grouped = e_pool.tile([P, GROUP * 512], BF16, align_bytes=64, name="e_grouped")
+            grouped = e_pool.tile([P, GROUP * PASS], BF16, align_bytes=64, name="e_grouped")
             grouped_words = grouped.bitcast(F32).rearrange("x (g r u) -> x g r u", g=GROUP, u=2)
             for first in range(0, passes, 2):
                 pair = min(2, passes - first)
@@ -288,8 +236,7 @@ def tile_trittentioncube_pb_kernel(tc, a_heads, step2, v_pairs, W_out, b_out, ou
                     for u in range(2):
                         start_word = 256 * (first + g) + P * u
                         nc.tensor.transpose(t_ps[:, g, u, :], e_words[:, start_word : start_word + P], ident_f32)
-                copy_out = nc.vector.tensor_copy if first == 0 else nc.scalar.copy
-                copy_out(
+                nc.scalar.copy(
                     out=grouped_words[:, first : first + pair],
                     in_=t_ps[:, 0:pair].rearrange("x g u r -> x g r u"),
                 )
@@ -301,12 +248,9 @@ def tile_trittentioncube_pb_kernel(tc, a_heads, step2, v_pairs, W_out, b_out, ou
             nc.vector.quantize_mx(
                 out=codes[:, 0 : passes * P].bitcast(FP8X4),
                 scales=scales[:, 0 : passes * P],
-                in_=grouped[:, 0 : passes * 512],
+                in_=grouped[:, 0 : passes * PASS],
             )
             return codes, scales
-
-        def passes_of(i):
-            return 1 if units[i][1] == MASKED else GROUP
 
         def multiply_stage(i):
             n, ci, half = units[i]
@@ -328,7 +272,7 @@ def tile_trittentioncube_pb_kernel(tc, a_heads, step2, v_pairs, W_out, b_out, ou
                 one = slice(n, n + 1)
                 nc.vector.tensor_reduce(out=total[:, one], in_=sums[:, n, :], axis=AX.X, op=ALU.add)
                 nc.vector.scalar_tensor_tensor(
-                    out=total[:, one], in0=e_fill[:, one], scalar=float(N_MASKED), in1=total[:, one],
+                    out=total[:, one], in0=sums[:, n, per_head - 1 : per_head], scalar=float(QUADS - 1), in1=total[:, one],
                     op0=ALU.mult, op1=ALU.add,
                 )
                 nc.vector.reciprocal(out=recip[:, one], in_=total[:, one])
@@ -338,7 +282,7 @@ def tile_trittentioncube_pb_kernel(tc, a_heads, step2, v_pairs, W_out, b_out, ou
             load_v(0)
 
             for bank in range(4):
-                d_ps = ps_s.tile([P, 512], F32, name="s_ps")
+                d_ps = ps_s.tile([P, PASS], F32, name="s_ps")
                 d_cells = d_ps.rearrange("r (n s u j h e) -> r n s u j h e", n=HEADS, s=4, u=2, j=4, h=2)
                 for s_in in range(4):
                     for h in range(2):
@@ -354,46 +298,46 @@ def tile_trittentioncube_pb_kernel(tc, a_heads, step2, v_pairs, W_out, b_out, ou
                 nc.vector.tensor_tensor(
                     out=diag_s[:, :, 4 * bank : 4 * bank + 4, :],
                     in0=d_ps.rearrange("r (n s x) -> r n s x", n=HEADS, s=4),
-                    in1=bound.unsqueeze(1).unsqueeze(1).to_broadcast([P, HEADS, 4, 32]),
+                    in1=ceiling.unsqueeze(1).unsqueeze(1).to_broadcast([P, HEADS, 4, 32]),
                     op=ALU.min,
                 )
+            nc.vector.tensor_tensor(
+                out=diag_s.rearrange("r n s x -> r (n s) x"),
+                in0=diag_s.rearrange("r n s x -> r (n s) x"),
+                in1=floor.unsqueeze(1).to_broadcast([P, HEADS * 16, 32]),
+                op=ALU.max,
+            )
             nc.vector.tensor_reduce(
-                out=part_max[:, :, STAT_COLS - 1 : STAT_COLS],
+                out=part_max[:, :, diag_col : diag_col + 1],
                 in_=diag_s.rearrange("r n s x -> r n (s x)"),
                 axis=AX.X,
                 op=ALU.max,
             )
 
-            for k, (ci, quad) in enumerate(scored):
-                scores_and_maximum(0, ci, quad)
-                if k % 6 == 0:
-                    step_v(k // 6)
-            statistics_of(0)
-            diagonal_blocks_of(0)
+            for k in range(per_head - 1):
+                scores_and_maximum(0, units[k][1], units[k][2])
+                if k < len(CHUNKS):
+                    step_v(k)
+            maximum_of(0)
 
             for i in range(len(units) + 3):
+                weave = i < len(units) - per_head
+                if weave and i % per_head > 0:
+                    scores_and_maximum(units[i][0] + 1, units[i - 1][1], units[i - 1][2])
+                    if i % per_head == per_head - 1:
+                        maximum_of(units[i][0] + 1)
                 if i < len(units):
                     exp_stage(i)
                 if 0 <= i - 1 < len(units):
                     e_grouped[i - 1] = transpose_rows(e_rows[i - 1].bitcast(F32), passes_of(i - 1))
                 if 0 <= i - 2 < len(units):
                     e_codes[i - 2] = quantise_rows(e_grouped[i - 2], passes_of(i - 2))
-                if i < len(units) - per_head:
-                    n, ci, half = units[i]
-                    k = i % per_head
-                    for quad in range(GROUP * half, GROUP * (half + 1)):
-                        if (ci, quad) in kept_cols:
-                            scores_and_maximum(n + 1, ci, quad)
-                    if k % 2 == 0:
-                        step_v(len(CHUNKS) * (n + 1) + k // 2)
-                    if k == per_head - 1:
-                        statistics_of(n + 1)
-                if i == len(units) - per_head:
+                if i % 2 == 0 and i // 2 + len(CHUNKS) < len(v_order):
+                    step_v(i // 2 + len(CHUNKS))
+                if i % 2 == 0 and i // 2 + len(CHUNKS) == len(v_order):
                     quantise_v(len(v_order) - 1)
                 if 0 <= i - 3:
                     multiply_stage(i - 3)
-                if i < len(units) - per_head and i % per_head == per_head - 1:
-                    diagonal_blocks_of(i // per_head + 1)
 
             z_codes, z_scales = quantise_rows(transpose_rows(z_bf.bitcast(F32), 1), 1)
             o_ps = ps_s.tile([P, 512], F32, name="s_ps")

@@ -17,180 +17,213 @@ HEADS = 4
 FILL = 1e-6
 INV_DH = 1.0 / 128.0
 BIG = 1e30
-ROWS = 64
-QUADS = 8
-GROUP = 4
+ROWS = 32
+SLOTS = 16
 PASS = 512
+QUADS = 4
+UNIT = QUADS * PASS
 
-LIVE, DIAG_A, DIAG_B, MASKED = 0, 1, 2, 3
-CHUNKS = (((0, 64), (0, 96)), ((0, 0), (64, 64)), ((0, 32), (64, 96)), ((64, 0), (64, 32)))
-V_ON_VECTOR = 6
+FULL_A = ((0, 64), (32, 64), (0, 32), (64, 96))
+FULL_B = ((0, 80), (32, 80), (0, 48), (64, 112))
+FULL_C = ((0, 96), (32, 96), (0, 112), (32, 112))
+DIAG_A = ((0, 0), (32, 32), (64, 64), (96, 96))
+DIAG_B = ((0, 16), (32, 48), (64, 80), (96, 112))
+MASK_A = ((64, 0), (96, 0), (32, 0), (96, 64))
+MASK_B = ((64, 16), (96, 16), (32, 16), (96, 80))
+MASK_C = ((64, 32), (96, 32), (64, 48), (96, 48))
+LIVE_UNITS = (FULL_A, FULL_B, FULL_C, DIAG_A, DIAG_B)
+MASK_UNITS = (MASK_A, MASK_B, MASK_C)
+V_UNITS = MASK_UNITS + LIVE_UNITS
+LIVE = len(LIVE_UNITS)
+MASKED_PAIRS = len(MASK_UNITS) * UNIT
+CONST = 256
 
 FLOPS = 2 * 128 * 512 * 128 * 128 + 2 * 4 * 128 * 16384 * 128 + 2 * 128 * 512 * 512
 
 
-def rows_below_diagonal(ci, quad):
-    p0, q0 = CHUNKS[ci][0]
-    return min(ROWS, max(0, q0 - p0 + 4 * quad))
+def live_rows(k, g):
+    if LIVE_UNITS[k] == DIAG_A:
+        return 4 * g
+    if LIVE_UNITS[k] == DIAG_B:
+        return SLOTS + 4 * g
+    return ROWS
 
 
 def tile_trittentioncube_pb_kernel(tc, a_heads, step2, v_pairs, W_out, b_out, out):
     nc = tc.nc
     v_plane = v_pairs.rearrange("n (p q) f -> n p q f", q=P)
-    kept_passes = 3 * QUADS
-    diag_col = kept_passes
+    passes = LIVE * QUADS
 
     with ExitStack() as stack:
+        stack.enter_context(tc.manual_schedule())
         keep = stack.enter_context(tc.tile_pool(name="keep", bufs=1))
-
-        ident_bf = keep.tile([P, P], BF16)
-        make_identity(nc, ident_bf)
-        ident_f32 = keep.tile([P, P], F32)
-        make_identity(nc, ident_f32)
+        stream = stack.enter_context(tc.tile_pool(name="stream", bufs=3))
+        codes_pool = stack.enter_context(tc.tile_pool(name="codes_pool", bufs=14))
+        e_pool = stack.enter_context(tc.tile_pool(name="e_pool", bufs=3))
 
         a_t = keep.tile([P, HEADS, P], BF16)
         s2 = keep.tile([P, P, P], BF16)
+        w_rows = keep.tile([P, 4, 512], BF16)
+        w_grouped = keep.tile([P, 2048], BF16, align_bytes=64)
         w_codes = keep.tile([P, 512], U32, align_bytes=64)
         w_scales = keep.tile([P, 512], U8, align_bytes=64)
         bias_rows = keep.tile([P, 512], BF16)
-        v_codes = keep.tile([P, HEADS, len(CHUNKS), QUADS, P], U32, align_bytes=64)
-        v_scales = keep.tile([P, HEADS, len(CHUNKS), QUADS, P], U8, align_bytes=64)
-        s_kept = keep.tile([P, kept_passes * PASS + 256], F32)
-        part_max = keep.tile([P, HEADS, kept_passes + 1], F32)
-        sums = keep.tile([P, HEADS, 7], F32)
+        d_kept = [keep.tile([P, 2 * UNIT + 8 * 32], F32, name="d_kept%d" % k) for k in range(2)]
+        part_max = keep.tile([P, HEADS, passes + 1], F32)
+        sums = keep.tile([P, HEADS, LIVE + 1], F32)
         top = keep.tile([P, HEADS], F32)
         neg_m = keep.tile([P, HEADS], F32)
         total = keep.tile([P, HEADS], F32)
         recip = keep.tile([P, HEADS], F32)
         fill_col = keep.tile([P, 1], F32)
-        ceiling = keep.tile([P, 32], F32)
-        floor = keep.tile([P, 32], F32)
-        diag_s = keep.tile([P, HEADS, 16, 32], F32)
+        warm = keep.tile([P, 1], F32)
+        ceiling = keep.tile([P, 64], F32)
+        floor = keep.tile([P, 64], F32)
+        diag_s = keep.tile([P, HEADS, 8, 64], F32)
         z_bf = keep.tile([P, HEADS * P], BF16)
+        o_sb = keep.tile([P, 512], F32)
 
-        nc.gpsimd.memset(s_kept[:, QUADS * PASS : kept_passes * PASS], FILL)
+        ident_bf = keep.tile([P, P], BF16)
+        make_identity(nc, ident_bf)
+        ident_f32 = keep.tile([P, P], F32)
+        make_identity(nc, ident_f32)
+        for k in range(2):
+            nc.gpsimd.memset(d_kept[k], FILL)
         nc.vector.memset(fill_col, FILL)
         nc.vector.memset(part_max, FILL)
+        nc.scalar.activation(out=warm, in_=fill_col, func=ACT.Exp)
         nc.vector.memset(ceiling, -BIG)
         nc.vector.memset(floor, FILL)
         for t in range(1, 4):
             for cells, value in ((ceiling, BIG), (floor, -BIG)):
                 nc.vector.memset(
-                    cells.rearrange("r (u j h e) -> r u j h e", u=2, j=4, h=2)[:, t // 2, 0:t, :, t % 2], value
+                    cells.rearrange("r (u i b e) -> r u i b e", u=2, i=4, b=4)[:, t // 2, 0:t, :, t % 2], value
                 )
+
+        v_order = [(n, j) for n in range(HEADS) for j in range(len(V_UNITS))]
+        v_raw = {}
+        v_grouped = {}
+        v_codes = {}
+
+        def load_v(k):
+            if k < len(v_order):
+                n, j = v_order[k]
+                v_raw[k] = stream.tile([P, SLOTS, P], BF16, name="v_raw", bufs=5)
+                for b, (p0, q0) in enumerate(V_UNITS[j]):
+                    nc.sync.dma_start(out=v_raw[k][b:P:4, :, :], in_=v_plane[n, p0 : p0 + ROWS, q0 : q0 + SLOTS, :])
+
+        def regroup_v(k, cut):
+            v_grouped[k] = stream.tile([P, QUADS, P, 4], BF16, align_bytes=64, name="v_grouped", bufs=5)
+            for first, last, copy in ((0, cut, nc.vector.tensor_copy), (cut, P, nc.scalar.copy)):
+                if first < last:
+                    copy(
+                        out=v_grouped[k][:, :, first:last].rearrange("x g (c i) t -> x g c t i", i=4),
+                        in_=v_raw[k][:, :, first:last].rearrange("x (g t) (c i) -> x g c t i", t=4, i=4),
+                    )
+
+        def quantise_v(k):
+            n, j = v_order[k]
+            codes = codes_pool.tile([P, QUADS * P], U32, align_bytes=64, name="v_codes")
+            scales = codes_pool.tile([P, QUADS * P], U8, align_bytes=64, name="v_scales")
+            nc.vector.quantize_mx(
+                out=codes.bitcast(FP8X4), scales=scales, in_=v_grouped[k].rearrange("x g f t -> x (g f t)")
+            )
+            v_codes[n, j] = (codes, scales)
+
+        def step_v(k, cut):
+            if 0 < k <= len(v_order):
+                quantise_v(k - 1)
+            if k < len(v_order):
+                regroup_v(k, cut)
+                load_v(k + 5)
 
         with tc.tile_pool(name="early", bufs=1) as early, tc.psum_pool(name="ps_early", bufs=1) as ps_early:
             a_rows = early.tile([P, HEADS * P], BF16)
             nc.sync.dma_start(out=a_rows, in_=a_heads.rearrange("p n i -> p (n i)"))
-            w_rows = early.tile([P, 4, 512], BF16)
-            nc.sync.dma_start(out=w_rows, in_=W_out.rearrange("(c o) k -> o c k", o=P))
             s_raw = early.tile([P, P, P], BF16)
             for rc in range(8):
                 r_cols = slice(16 * rc, 16 * rc + 16)
                 nc.sync.dma_start(out=s_raw[:, r_cols, :], in_=step2[r_cols].rearrange("r i q -> i r q"))
-            nc.sync.dma_start(out=bias_rows, in_=b_out.partition_broadcast(P))
+            for k in range(2):
+                load_v(k)
+            nc.sync.dma_start(out=w_rows, in_=W_out.rearrange("(c o) k -> o c k", o=P))
+            for k in range(2, 5):
+                load_v(k)
 
             a_ps = ps_early.tile([P, HEADS, P], BF16)
             for n in range(HEADS):
                 nc.tensor.transpose(a_ps[:, n, :], a_rows[:, n * P : (n + 1) * P], ident_bf)
             nc.vector.tensor_copy(out=a_t, in_=a_ps)
 
-            w_words = w_rows.bitcast(F32)
-            w_grouped = early.tile([P, 2048], BF16, align_bytes=64)
-            w_grouped_words = w_grouped.bitcast(F32).rearrange("x (c o u) -> x c o u", c=4, u=2)
-            for half in range(2):
-                w_ps = ps_early.tile([P, 2, 2, P], F32, bufs=2)
-                for c in range(2):
-                    for u in range(2):
-                        nc.tensor.transpose(w_ps[:, c, u, :], w_words[:, 2 * half + c, u * P : (u + 1) * P], ident_f32)
-                nc.vector.tensor_copy(
-                    out=w_grouped_words[:, 2 * half : 2 * half + 2], in_=w_ps.rearrange("x c u o -> x c o u")
-                )
-            nc.vector.quantize_mx(out=w_codes.bitcast(FP8X4), scales=w_scales, in_=w_grouped)
-
+            cut = 80
             for rc in range(8):
                 r_cols = slice(16 * rc, 16 * rc + 16)
                 src = s_raw[:, r_cols, :].rearrange("i r q -> i q r")
-                if rc % 2 == 0 and rc < 6:
-                    nc.scalar.copy(out=s2[:, :, r_cols], in_=src)
-                else:
-                    nc.vector.tensor_copy(out=s2[:, :, r_cols], in_=src)
+                nc.vector.tensor_copy(out=s2[:, 0:cut, r_cols], in_=src[:, 0:cut, :])
+                nc.scalar.copy(out=s2[:, cut:P, r_cols], in_=src[:, cut:P, :])
 
-        stream = stack.enter_context(tc.tile_pool(name="stream", bufs=2))
-        e_pool = stack.enter_context(tc.tile_pool(name="e_pool", bufs=2))
-        ps_s = stack.enter_context(tc.psum_pool(name="ps_s", bufs=4))
-        ps_t = stack.enter_context(tc.psum_pool(name="ps_t", bufs=2))
+        kept = stack.enter_context(tc.tile_pool(name="kept", bufs=4))
+        ps_s = stack.enter_context(tc.psum_pool(name="ps_s", bufs=3))
+        ps_t = stack.enter_context(tc.psum_pool(name="ps_t", bufs=3))
         ps_z = stack.enter_context(tc.psum_pool(name="ps_z", bufs=2))
 
-        v_order = [(n, ci) for n in range(HEADS) for ci in range(len(CHUNKS))]
-        v_raw = {}
-        v_grouped = {}
+        s_kept = {}
 
-        def load_v(k):
-            if k < len(v_order):
-                n, ci = v_order[k]
-                v_raw[k] = stream.tile([P, 4 * QUADS, P], BF16, name="v_raw")
-                for h, (p0, q0) in enumerate(CHUNKS[ci]):
-                    nc.sync.dma_start(out=v_raw[k][h:P:2, :, :], in_=v_plane[n, p0 : p0 + ROWS, q0 : q0 + 4 * QUADS, :])
-
-        def regroup_v(k):
-            v_grouped[k] = stream.tile([P, QUADS, P, 4], BF16, align_bytes=64, name="v_grouped")
-            cut = V_ON_VECTOR
-            nc.vector.tensor_copy(
-                out=v_grouped[k][:, 0:cut].rearrange("x j (c i) t -> x j c t i", i=4),
-                in_=v_raw[k][:, 0 : 4 * cut, :].rearrange("x (j t) (c i) -> x j c t i", t=4, i=4),
-            )
-            nc.scalar.copy(
-                out=v_grouped[k][:, cut:QUADS], in_=v_raw[k][:, 4 * cut : 4 * QUADS, :].rearrange("x (j t) f -> x j f t", t=4)
-            )
-
-        def quantise_v(k):
-            n, ci = v_order[k]
-            nc.vector.quantize_mx(
-                out=v_codes[:, n, ci].rearrange("x j f -> x (j f)").bitcast(FP8X4),
-                scales=v_scales[:, n, ci].rearrange("x j f -> x (j f)"),
-                in_=v_grouped[k].rearrange("x j f t -> x (j f t)"),
-            )
-
-        def step_v(k):
-            load_v(k + 1)
-            if k > 0:
-                quantise_v(k - 1)
-            regroup_v(k)
-
-        def scores_and_maximum(n, ci, half):
-            for quad in range(GROUP * half, GROUP * (half + 1)):
-                rows = rows_below_diagonal(ci, quad)
+        def scores_and_maximum(n, k):
+            corners = LIVE_UNITS[k]
+            if k < LIVE - 2:
+                s_kept[n, k] = kept.tile([P, UNIT], F32, name="s_kept")
+            else:
+                s_kept[n, k] = d_kept[n % 2][:, (k - LIVE + 2) * UNIT : (k - LIVE + 3) * UNIT]
+            for g in range(QUADS):
+                rows = live_rows(k, g)
                 if rows > 0:
-                    s_ps = ps_s.tile([P, PASS], F32)
-                    cells = s_ps[:, 0 : 8 * rows].rearrange("r (u p h e) -> r u p h e", u=2, h=2, e=2)
-                    for h, (p0, q0) in enumerate(CHUNKS[ci]):
-                        for t in range(4):
+                    s_ps = ps_s.tile([P, PASS], F32, name="s_ps")
+                    cells = s_ps.rearrange("r (u b e i) -> r u b e i", u=2, b=4, e=2)
+                    for t in range(4):
+                        b = 0
+                        while b < 4:
+                            p0, q0 = corners[b]
+                            wide = 2 if rows == ROWS and b < 3 and corners[b + 1] == (p0 + ROWS, q0) else 1
                             nc.tensor.matmul(
-                                out=cells[:, t // 2, :, h, t % 2],
-                                lhsT=s2[:, q0 + 4 * quad + t, :],
-                                rhs=a_t[:, n, p0 : p0 + rows],
+                                out=cells[:, t // 2, b : b + wide, t % 2, 0:rows],
+                                lhsT=s2[:, q0 + 4 * g + t, :],
+                                rhs=a_t[:, n, p0 : p0 + wide * rows].rearrange("i (b p) -> i b p", b=wide),
                                 start=True,
                                 stop=True,
                             )
-                    kept = QUADS * ci + quad
+                            b += wide
                     nc.vector.tensor_scalar(
-                        out=s_kept[:, kept * PASS : (kept + 1) * PASS].rearrange("r (u x) -> r u x", u=2)[:, :, 0 : 4 * rows],
-                        in0=s_ps[:, 0 : 8 * rows].rearrange("r (u x) -> r u x", u=2),
+                        out=s_kept[n, k][:, g * PASS : (g + 1) * PASS]
+                        .rearrange("r (u i c) -> r u i c", u=2, c=8)[:, :, 0:rows, :],
+                        in0=s_ps.rearrange("r (u c i) -> r u i c", u=2, c=8)[:, :, 0:rows, :],
                         scalar1=1.0,
                         scalar2=None,
                         op0=ALU.mult,
                         op1=ALU.max,
-                        accum_out=part_max[:, n, kept : kept + 1],
+                        accum_out=part_max[:, n, QUADS * k + g : QUADS * k + g + 1],
                     )
-            if ci != LIVE:
-                s0 = rows_below_diagonal(ci, GROUP * half) // 4
-                first = QUADS * PASS + (PASS + 16) * s0
+            if k == LIVE - 2:
+                nc.vector.tensor_tensor(
+                    out=diag_s[:, n],
+                    in0=diag_s[:, n],
+                    in1=floor.unsqueeze(1).to_broadcast([P, 8, 64]),
+                    op=ALU.max,
+                )
+                nc.vector.tensor_reduce(
+                    out=part_max[:, n, passes : passes + 1],
+                    in_=diag_s[:, n].rearrange("r s x -> r (s x)"),
+                    axis=AX.X,
+                    op=ALU.max,
+                )
+            if k >= LIVE - 2:
+                half = k - LIVE + 2
+                first = half * (UNIT + 128)
                 nc.vector.tensor_copy(
-                    out=s_kept[:, first : first + GROUP * (PASS + 16)]
-                    .rearrange("r (g y) -> r g y", g=GROUP)[:, :, 0:PASS]
-                    .rearrange("r g (u x) -> r g u x", u=2)[:, :, :, 0:16],
-                    in_=diag_s[:, n, s0 : s0 + GROUP, :].rearrange("r g (u x) -> r g u x", u=2),
+                    out=d_kept[n % 2][:, first : first + QUADS * (PASS + 32)]
+                    .rearrange("r (g y) -> r g y", g=QUADS)[:, :, 0:PASS]
+                    .rearrange("r g (u x) -> r g u x", u=2)[:, :, :, 0:32],
+                    in_=diag_s[:, n, QUADS * half : QUADS * (half + 1), :].rearrange("r g (u x) -> r g u x", u=2),
                 )
 
         def maximum_of(n):
@@ -198,158 +231,193 @@ def tile_trittentioncube_pb_kernel(tc, a_heads, step2, v_pairs, W_out, b_out, ou
             nc.vector.tensor_reduce(out=top[:, one], in_=part_max[:, n, :], axis=AX.X, op=ALU.max)
             nc.vector.tensor_scalar(out=neg_m[:, one], in0=top[:, one], scalar1=-INV_DH, scalar2=None, op0=ALU.mult)
 
-        units = [
-            (n, ci, half)
-            for n in range(HEADS)
-            for ci, half in ((LIVE, 0), (LIVE, 1), (DIAG_A, 0), (DIAG_A, 1), (DIAG_B, 0), (DIAG_B, 1), (MASKED, 0))
-        ]
-        per_head = len(units) // HEADS
         e_rows = {}
         e_grouped = {}
         e_codes = {}
         z_ps = {}
 
-        def passes_of(i):
-            return 1 if units[i][1] == MASKED else GROUP
-
-        def exp_stage(i):
-            n, ci, half = units[i]
-            width = passes_of(i) * PASS
-            first = (QUADS * ci + GROUP * half) * PASS
-            e_rows[i] = e_pool.tile([P, GROUP * PASS], BF16, name="e_rows")
+        def exp_const(n):
+            e_rows[n, -1] = e_pool.tile([P, CONST], BF16, name="e_const_rows", bufs=1)
             nc.scalar.activation(
-                out=e_rows[i][:, 0:width],
-                in_=fill_col.to_broadcast([P, width]) if ci == MASKED else s_kept[:, first : first + width],
+                out=e_rows[n, -1],
+                in_=fill_col.to_broadcast([P, CONST]),
                 func=ACT.Exp,
                 bias=neg_m[:, n : n + 1],
                 scale=INV_DH,
-                accum_out=sums[:, n, i % per_head : i % per_head + 1],
+                accum_out=sums[:, n, LIVE : LIVE + 1],
             )
 
-        def transpose_rows(e_words, passes):
-            grouped = e_pool.tile([P, GROUP * PASS], BF16, align_bytes=64, name="e_grouped")
-            grouped_words = grouped.bitcast(F32).rearrange("x (g r u) -> x g r u", g=GROUP, u=2)
-            for first in range(0, passes, 2):
-                pair = min(2, passes - first)
-                t_ps = ps_t.tile([P, 2, 2, P], F32)
+        def exp_stage(n, k):
+            e_rows[n, k] = e_pool.tile([P, UNIT], BF16, name="e_rows")
+            nc.scalar.activation(
+                out=e_rows[n, k],
+                in_=s_kept[n, k],
+                func=ACT.Exp,
+                bias=neg_m[:, n : n + 1],
+                scale=INV_DH,
+                accum_out=sums[:, n, k : k + 1],
+            )
+
+        def transpose_rows(words, count, copy):
+            grouped = e_pool.tile([P, UNIT], BF16, align_bytes=64, name="e_grouped")
+            grouped_words = grouped.bitcast(F32).rearrange("x (g r u) -> x g r u", g=QUADS, u=2)
+            for first in range(0, count, 2):
+                pair = min(2, count - first)
+                t_ps = ps_t.tile([P, 2, 2, P], F32, name="t_ps")
                 for g in range(pair):
                     for u in range(2):
                         start_word = 256 * (first + g) + P * u
-                        nc.tensor.transpose(t_ps[:, g, u, :], e_words[:, start_word : start_word + P], ident_f32)
-                nc.scalar.copy(
-                    out=grouped_words[:, first : first + pair],
-                    in_=t_ps[:, 0:pair].rearrange("x g u r -> x g r u"),
-                )
+                        nc.tensor.transpose(t_ps[:, g, u, :], words[:, start_word : start_word + P], ident_f32)
+                copy(out=grouped_words[:, first : first + pair], in_=t_ps[:, 0:pair].rearrange("x g u r -> x g r u"))
             return grouped
 
-        def quantise_rows(grouped, passes):
-            codes = e_pool.tile([P, GROUP * P], U32, align_bytes=64, name="e_codes")
-            scales = e_pool.tile([P, GROUP * P], U8, align_bytes=64, name="e_scales")
+        def transpose_const(n):
+            grouped = e_pool.tile([P, PASS], BF16, align_bytes=64, name="e_const_grouped", bufs=1)
+            t_ps = ps_t.tile([P, 2, 2, P], F32, name="t_ps")
+            nc.tensor.transpose(t_ps[:, 0, 0, :], e_rows[n, -1].bitcast(F32), ident_f32)
+            nc.scalar.copy(
+                out=grouped.bitcast(F32).rearrange("x (r u) -> x r u", u=2),
+                in_=t_ps[:, 0, 0, :].unsqueeze(2).to_broadcast([P, P, 2]),
+            )
+            return grouped
+
+        def quantise_rows(grouped, count):
+            codes = e_pool.tile([P, QUADS * P], U32, align_bytes=64, name="e_codes")
+            scales = e_pool.tile([P, QUADS * P], U8, align_bytes=64, name="e_scales")
             nc.vector.quantize_mx(
-                out=codes[:, 0 : passes * P].bitcast(FP8X4),
-                scales=scales[:, 0 : passes * P],
-                in_=grouped[:, 0 : passes * PASS],
+                out=codes[:, 0 : count * P].bitcast(FP8X4),
+                scales=scales[:, 0 : count * P],
+                in_=grouped[:, 0 : count * PASS],
             )
             return codes, scales
 
-        def multiply_stage(i):
-            n, ci, half = units[i]
-            codes, scales = e_codes[i]
-            if i % per_head == 0:
-                z_ps[n] = ps_z.tile([P, P], F32, name="z_ps")
-            for quad in range(QUADS) if ci == MASKED else range(GROUP * half, GROUP * (half + 1)):
-                g = 0 if ci == MASKED else quad - GROUP * half
-                nc.tensor.matmul_mx(
-                    out=z_ps[n],
-                    lhsT=codes[:, g * P : (g + 1) * P].bitcast(FP8X4),
-                    lhsT_scale=scales[:, g * P : (g + 1) * P],
-                    rhs=v_codes[:, n, ci, quad, :].bitcast(FP8X4),
-                    rhs_scale=v_scales[:, n, ci, quad, :],
-                    start=(ci == 0 and quad == 0),
-                    stop=(ci == len(CHUNKS) - 1 and quad == QUADS - 1),
-                )
-            if i % per_head == per_head - 1:
-                one = slice(n, n + 1)
-                nc.vector.tensor_reduce(out=total[:, one], in_=sums[:, n, :], axis=AX.X, op=ALU.add)
-                nc.vector.scalar_tensor_tensor(
-                    out=total[:, one], in0=sums[:, n, per_head - 1 : per_head], scalar=float(QUADS - 1), in1=total[:, one],
-                    op0=ALU.mult, op1=ALU.add,
-                )
-                nc.vector.reciprocal(out=recip[:, one], in_=total[:, one])
-                nc.scalar.activation(out=z_bf[:, n * P : (n + 1) * P], in_=z_ps[n], func=ACT.Copy, scale=recip[:, one])
+        def quantise_const(grouped):
+            codes = e_pool.tile([P, P], U32, align_bytes=64, name="e_const_codes", bufs=2)
+            scales = e_pool.tile([P, P], U8, align_bytes=64, name="e_const_scales", bufs=2)
+            nc.vector.quantize_mx(out=codes.bitcast(FP8X4), scales=scales, in_=grouped)
+            return codes, scales
 
-        with tc.manual_schedule():
-            load_v(0)
-
-            for bank in range(4):
-                d_ps = ps_s.tile([P, PASS], F32, name="s_ps")
-                d_cells = d_ps.rearrange("r (n s u j h e) -> r n s u j h e", n=HEADS, s=4, u=2, j=4, h=2)
-                for s_in in range(4):
-                    for h in range(2):
-                        corner = 64 * h + 4 * (4 * bank + s_in)
-                        for t in range(4):
-                            nc.tensor.matmul(
-                                out=d_cells[:, :, s_in, t // 2, :, h, t % 2],
-                                lhsT=s2[:, corner + t, :],
-                                rhs=a_t[:, :, corner : corner + 4],
-                                start=True,
-                                stop=True,
-                            )
-                nc.vector.tensor_tensor(
-                    out=diag_s[:, :, 4 * bank : 4 * bank + 4, :],
-                    in0=d_ps.rearrange("r (n s x) -> r n s x", n=HEADS, s=4),
-                    in1=ceiling.unsqueeze(1).unsqueeze(1).to_broadcast([P, HEADS, 4, 32]),
-                    op=ALU.min,
-                )
-            nc.vector.tensor_tensor(
-                out=diag_s.rearrange("r n s x -> r (n s) x"),
-                in0=diag_s.rearrange("r n s x -> r (n s) x"),
-                in1=floor.unsqueeze(1).to_broadcast([P, HEADS * 16, 32]),
-                op=ALU.max,
-            )
-            nc.vector.tensor_reduce(
-                out=part_max[:, :, diag_col : diag_col + 1],
-                in_=diag_s.rearrange("r n s x -> r n (s x)"),
-                axis=AX.X,
-                op=ALU.max,
-            )
-
-            for k in range(per_head - 1):
-                scores_and_maximum(0, units[k][1], units[k][2])
-                if k < len(CHUNKS):
-                    step_v(k)
-            maximum_of(0)
-
-            for i in range(len(units) + 3):
-                weave = i < len(units) - per_head
-                if weave and i % per_head > 0:
-                    scores_and_maximum(units[i][0] + 1, units[i - 1][1], units[i - 1][2])
-                    if i % per_head == per_head - 1:
-                        maximum_of(units[i][0] + 1)
-                if i < len(units):
-                    exp_stage(i)
-                if 0 <= i - 1 < len(units):
-                    e_grouped[i - 1] = transpose_rows(e_rows[i - 1].bitcast(F32), passes_of(i - 1))
-                if 0 <= i - 2 < len(units):
-                    e_codes[i - 2] = quantise_rows(e_grouped[i - 2], passes_of(i - 2))
-                if i % 2 == 0 and i // 2 + len(CHUNKS) < len(v_order):
-                    step_v(i // 2 + len(CHUNKS))
-                if i % 2 == 0 and i // 2 + len(CHUNKS) == len(v_order):
-                    quantise_v(len(v_order) - 1)
-                if 0 <= i - 3:
-                    multiply_stage(i - 3)
-
-            z_codes, z_scales = quantise_rows(transpose_rows(z_bf.bitcast(F32), 1), 1)
-            o_ps = ps_s.tile([P, 512], F32, name="s_ps")
+        def add_pass(n, e_pair, g, v_pair, h, first, last):
             nc.tensor.matmul_mx(
-                out=o_ps,
-                lhsT=z_codes[:, 0:P].bitcast(FP8X4),
-                lhsT_scale=z_scales[:, 0:P],
-                rhs=w_codes.bitcast(FP8X4),
-                rhs_scale=w_scales,
-                start=True,
-                stop=True,
+                out=z_ps[n],
+                lhsT=e_pair[0][:, g * P : (g + 1) * P].bitcast(FP8X4),
+                lhsT_scale=e_pair[1][:, g * P : (g + 1) * P],
+                rhs=v_pair[0][:, h * P : (h + 1) * P].bitcast(FP8X4),
+                rhs_scale=v_pair[1][:, h * P : (h + 1) * P],
+                start=first,
+                stop=last,
             )
-            o_sb = keep.tile([P, 512], F32)
-            nc.vector.tensor_tensor(out=o_sb, in0=o_ps, in1=bias_rows, op=ALU.add)
-            nc.sync.dma_start(out=out, in_=o_sb)
+
+        def multiply_stage(n, k):
+            if k == 0:
+                z_ps[n] = ps_z.tile([P, P], F32, name="z_ps")
+                for j in range(len(MASK_UNITS)):
+                    for h in range(QUADS):
+                        add_pass(n, e_codes[n, -1], 0, v_codes[n, j], h, j == 0 and h == 0, False)
+            for g in range(QUADS):
+                add_pass(n, e_codes[n, k], g, v_codes[n, len(MASK_UNITS) + k], g, False, k == LIVE - 1 and g == QUADS - 1)
+
+        def divisor_of(n):
+            one = slice(n, n + 1)
+            nc.vector.tensor_reduce(out=total[:, one], in_=sums[:, n, :], axis=AX.X, op=ALU.add)
+            nc.vector.scalar_tensor_tensor(
+                out=total[:, one], in0=sums[:, n, LIVE : LIVE + 1], scalar=float(MASKED_PAIRS // CONST - 1),
+                in1=total[:, one], op0=ALU.mult, op1=ALU.add,
+            )
+            nc.vector.reciprocal(out=recip[:, one], in_=total[:, one])
+
+        def finish_head(n):
+            nc.scalar.activation(
+                out=z_bf[:, n * P : (n + 1) * P], in_=z_ps[n], func=ACT.Copy, scale=recip[:, n : n + 1]
+            )
+
+        for bank in range(4):
+            d_ps = ps_s.tile([P, PASS], F32, name="s_ps")
+            d_cells = d_ps.rearrange("r (n s u i b e) -> r n s u i b e", n=HEADS, s=2, u=2, i=4, b=4)
+            for s_in in range(2):
+                for b in range(4):
+                    corner = ROWS * b + 4 * (2 * bank + s_in)
+                    for t in range(4):
+                        nc.tensor.matmul(
+                            out=d_cells[:, :, s_in, t // 2, :, b, t % 2],
+                            lhsT=s2[:, corner + t, :],
+                            rhs=a_t[:, :, corner : corner + 4],
+                            start=True,
+                            stop=True,
+                        )
+            nc.vector.tensor_tensor(
+                out=diag_s[:, :, 2 * bank : 2 * bank + 2, :],
+                in0=d_ps.rearrange("r (n s x) -> r n s x", n=HEADS, s=2),
+                in1=ceiling.unsqueeze(1).unsqueeze(1).to_broadcast([P, HEADS, 2, 64]),
+                op=ALU.min,
+            )
+
+        for k in range(LIVE):
+            scores_and_maximum(0, k)
+            regroup_v(k, 0)
+            load_v(k + 5)
+        maximum_of(0)
+        next_v = LIVE
+        for k in range(LIVE - 1):
+            quantise_v(k)
+
+        units = [(n, k) for n in range(HEADS) for k in range(LIVE)]
+        for i in range(len(units) + 3):
+            if i < len(units):
+                n, k = units[i]
+                if k == 0:
+                    exp_const(n)
+                exp_stage(n, k)
+            if 0 <= i - 2 < len(units):
+                n, k = units[i - 2]
+                if k == 0:
+                    e_codes[n, -1] = quantise_const(e_grouped[n, -1])
+                e_codes[n, k] = quantise_rows(e_grouped[n, k], QUADS)
+                if k == LIVE - 1:
+                    divisor_of(n)
+            if 0 <= i - 1 < len(units):
+                n, k = units[i - 1]
+                if k == 0:
+                    e_grouped[n, -1] = transpose_const(n)
+                e_grouped[n, k] = transpose_rows(e_rows[n, k].bitcast(F32), QUADS, nc.scalar.copy)
+            if i + LIVE < len(units):
+                n, k = units[i + LIVE]
+                scores_and_maximum(n, k)
+                if k == LIVE - 1:
+                    maximum_of(n)
+            for step in range(2 if i % 5 in (0, 2, 4) else 1):
+                step_v(next_v, P if i >= len(units) - LIVE else 64)
+                next_v += 1
+            if 0 <= i - 4 and units[i - 4][1] == LIVE - 1:
+                finish_head(units[i - 4][0])
+            if 0 <= i - 3:
+                multiply_stage(*units[i - 3])
+            if i == 1:
+                w_words = w_rows.bitcast(F32)
+                w_grouped_words = w_grouped.bitcast(F32).rearrange("x (c o u) -> x c o u", c=4, u=2)
+                for half in range(2):
+                    w_ps = ps_t.tile([P, 2, 2, P], F32, name="t_ps")
+                    for c in range(2):
+                        for u in range(2):
+                            nc.tensor.transpose(w_ps[:, c, u, :], w_words[:, 2 * half + c, u * P : (u + 1) * P], ident_f32)
+                    nc.vector.tensor_copy(
+                        out=w_grouped_words[:, 2 * half : 2 * half + 2], in_=w_ps.rearrange("x c u o -> x c o u")
+                    )
+            if i == 2:
+                nc.vector.quantize_mx(out=w_codes.bitcast(FP8X4), scales=w_scales, in_=w_grouped)
+                nc.sync.dma_start(out=bias_rows, in_=b_out.partition_broadcast(P))
+
+        finish_head(HEADS - 1)
+        z_codes, z_scales = quantise_rows(transpose_rows(z_bf.bitcast(F32), 1, nc.scalar.copy), 1)
+        o_ps = ps_s.tile([P, 512], F32, name="s_ps")
+        nc.tensor.matmul_mx(
+            out=o_ps,
+            lhsT=z_codes[:, 0:P].bitcast(FP8X4),
+            lhsT_scale=z_scales[:, 0:P],
+            rhs=w_codes.bitcast(FP8X4),
+            rhs_scale=w_scales,
+            start=True,
+            stop=True,
+        )
+        nc.vector.tensor_tensor(out=o_sb, in0=o_ps, in1=bias_rows, op=ALU.add)
+        nc.sync.dma_start(out=out, in_=o_sb)

@@ -114,8 +114,23 @@ def tile_trittentioncube_pb_kernel(tc, a_heads, step2, v_pairs, W_out, b_out, ou
 
         def regroup_v(k, cut):
             v_grouped[k] = stream.tile([P, QUADS, P, 4], BF16, align_bytes=64, name="v_grouped", bufs=5)
+            by_pe = 0 < cut < P
+            if by_pe:
+                v_ps = ps_v.tile([P, QUADS, P - cut, 4], BF16, name="v_ps")
+                for g in range(QUADS):
+                    nc.tensor.matmul(
+                        out=v_ps[:, g],
+                        lhsT=ident_bf,
+                        rhs=v_raw[k][:, 4 * g : 4 * g + 4, cut:P].rearrange("x t f -> x f t"),
+                        start=True,
+                        stop=True,
+                    )
+                nc.scalar.copy(
+                    out=v_grouped[k][:, :, cut:P].rearrange("x g f t -> x g (f t)"),
+                    in_=v_ps.rearrange("x g f t -> x g (f t)"),
+                )
             for first, last, copy in ((0, cut, nc.vector.tensor_copy), (cut, P, nc.scalar.copy)):
-                if first < last:
+                if first < last and not (by_pe and last == P):
                     copy(
                         out=v_grouped[k][:, :, first:last].rearrange("x g (c i) t -> x g c t i", i=4),
                         in_=v_raw[k][:, :, first:last].rearrange("x (g t) (c i) -> x g c t i", t=4, i=4),
@@ -164,8 +179,9 @@ def tile_trittentioncube_pb_kernel(tc, a_heads, step2, v_pairs, W_out, b_out, ou
 
         kept = stack.enter_context(tc.tile_pool(name="kept", bufs=4))
         ps_s = stack.enter_context(tc.psum_pool(name="ps_s", bufs=3))
-        ps_t = stack.enter_context(tc.psum_pool(name="ps_t", bufs=3))
-        ps_z = stack.enter_context(tc.psum_pool(name="ps_z", bufs=2))
+        ps_t = stack.enter_context(tc.psum_pool(name="ps_t", bufs=2))
+        ps_v = stack.enter_context(tc.psum_pool(name="ps_v", bufs=2))
+        ps_z = stack.enter_context(tc.psum_pool(name="ps_z", bufs=1))
 
         s_kept = {}
 

@@ -16,7 +16,6 @@ P = 128
 HEADS = 4
 FILL = 1e-6
 INV_DH = 1.0 / 128.0
-BIG = 1e30
 ROWS = 32
 SLOTS = 16
 PASS = 512
@@ -36,6 +35,12 @@ MASK_UNITS = (MASK_A, MASK_B, MASK_C)
 V_UNITS = MASK_UNITS + LIVE_UNITS
 LIVE = len(LIVE_UNITS)
 MASKED_PAIRS = len(MASK_UNITS) * UNIT
+V_RAW = 5
+V_FIRST = 2
+V_NUM, V_DEN = 5, 4
+W_ROUND = 14
+SHARED = False
+CUT, CUT_LAST = 64, P
 CONST = 256
 
 FLOPS = 2 * 128 * 512 * 128 * 128 + 2 * 4 * 128 * 16384 * 128 + 2 * 128 * 512 * 512
@@ -58,13 +63,11 @@ def tile_trittentioncube_pb_kernel(tc, a_heads, step2, v_pairs, W_out, b_out, ou
         stack.enter_context(tc.manual_schedule())
         keep = stack.enter_context(tc.tile_pool(name="keep", bufs=1))
         stream = stack.enter_context(tc.tile_pool(name="stream", bufs=3))
-        codes_pool = stack.enter_context(tc.tile_pool(name="codes_pool", bufs=14))
+        codes_pool = stack.enter_context(tc.tile_pool(name="codes_pool", bufs=12))
         e_pool = stack.enter_context(tc.tile_pool(name="e_pool", bufs=3))
 
         a_t = keep.tile([P, HEADS, P], BF16)
         s2 = keep.tile([P, P, P], BF16)
-        w_rows = keep.tile([P, 4, 512], BF16)
-        w_grouped = keep.tile([P, 2048], BF16, align_bytes=64)
         w_codes = keep.tile([P, 512], U32, align_bytes=64)
         w_scales = keep.tile([P, 512], U8, align_bytes=64)
         bias_rows = keep.tile([P, 512], BF16)
@@ -77,8 +80,8 @@ def tile_trittentioncube_pb_kernel(tc, a_heads, step2, v_pairs, W_out, b_out, ou
         recip = keep.tile([P, HEADS], F32)
         fill_col = keep.tile([P, 1], F32)
         warm = keep.tile([P, 1], F32)
-        ceiling = keep.tile([P, 64], F32)
-        floor = keep.tile([P, 64], F32)
+        live = keep.tile([P, 64], F32)
+        dead = keep.tile([P, 64], F32)
         diag_s = keep.tile([P, HEADS, 8, 64], F32)
         z_bf = keep.tile([P, HEADS * P], BF16)
         o_sb = keep.tile([P, 512], F32)
@@ -92,10 +95,10 @@ def tile_trittentioncube_pb_kernel(tc, a_heads, step2, v_pairs, W_out, b_out, ou
         nc.vector.memset(fill_col, FILL)
         nc.vector.memset(part_max, FILL)
         nc.scalar.activation(out=warm, in_=fill_col, func=ACT.Exp)
-        nc.vector.memset(ceiling, -BIG)
-        nc.vector.memset(floor, FILL)
+        nc.vector.memset(live, 0.0)
+        nc.vector.memset(dead, FILL)
         for t in range(1, 4):
-            for cells, value in ((ceiling, BIG), (floor, -BIG)):
+            for cells, value in ((live, 1.0), (dead, 0.0)):
                 nc.vector.memset(
                     cells.rearrange("r (u i b e) -> r u i b e", u=2, i=4, b=4)[:, t // 2, 0:t, :, t % 2], value
                 )
@@ -108,33 +111,36 @@ def tile_trittentioncube_pb_kernel(tc, a_heads, step2, v_pairs, W_out, b_out, ou
         def load_v(k):
             if k < len(v_order):
                 n, j = v_order[k]
-                v_raw[k] = stream.tile([P, SLOTS, P], BF16, name="v_raw", bufs=5)
+                v_raw[k] = stream.tile([P, SLOTS, P], BF16, name="v_raw", bufs=V_RAW)
                 for b, (p0, q0) in enumerate(V_UNITS[j]):
                     nc.sync.dma_start(out=v_raw[k][b:P:4, :, :], in_=v_plane[n, p0 : p0 + ROWS, q0 : q0 + SLOTS, :])
 
-        def regroup_v(k, cut):
-            v_grouped[k] = stream.tile([P, QUADS, P, 4], BF16, align_bytes=64, name="v_grouped", bufs=5)
-            by_pe = 0 < cut < P
-            if by_pe:
-                v_ps = ps_v.tile([P, QUADS, P - cut, 4], BF16, name="v_ps")
-                for g in range(QUADS):
+        def regroup_by_copy(k, first, last, copy):
+            if first < last:
+                copy(
+                    out=v_grouped[k][:, :, first:last].rearrange("x g (c i) t -> x g c t i", i=4),
+                    in_=v_raw[k][:, :, first:last].rearrange("x (g t) (c i) -> x g c t i", t=4, i=4),
+                )
+
+        def regroup_by_pe(k, first):
+            for half in range(2):
+                v_ps = ps_v.tile([P, 2, P - first, 4], BF16, name="v_ps")
+                for g in range(2):
+                    t_rows = slice(8 * half + 4 * g, 8 * half + 4 * g + 4)
                     nc.tensor.matmul(
                         out=v_ps[:, g],
                         lhsT=ident_bf,
-                        rhs=v_raw[k][:, 4 * g : 4 * g + 4, cut:P].rearrange("x t f -> x f t"),
+                        rhs=v_raw[k][:, t_rows, first:P].rearrange("x t f -> x f t"),
                         start=True,
                         stop=True,
                     )
                 nc.scalar.copy(
-                    out=v_grouped[k][:, :, cut:P].rearrange("x g f t -> x g (f t)"),
+                    out=v_grouped[k][:, 2 * half : 2 * half + 2, first:P].rearrange("x g f t -> x g (f t)"),
                     in_=v_ps.rearrange("x g f t -> x g (f t)"),
                 )
-            for first, last, copy in ((0, cut, nc.vector.tensor_copy), (cut, P, nc.scalar.copy)):
-                if first < last and not (by_pe and last == P):
-                    copy(
-                        out=v_grouped[k][:, :, first:last].rearrange("x g (c i) t -> x g c t i", i=4),
-                        in_=v_raw[k][:, :, first:last].rearrange("x (g t) (c i) -> x g c t i", t=4, i=4),
-                    )
+
+        def group_tile(k):
+            v_grouped[k] = stream.tile([P, QUADS, P, 4], BF16, align_bytes=64, name="v_grouped", bufs=5)
 
         def quantise_v(k):
             n, j = v_order[k]
@@ -145,24 +151,17 @@ def tile_trittentioncube_pb_kernel(tc, a_heads, step2, v_pairs, W_out, b_out, ou
             )
             v_codes[n, j] = (codes, scales)
 
-        def step_v(k, cut):
-            if 0 < k <= len(v_order):
-                quantise_v(k - 1)
-            if k < len(v_order):
-                regroup_v(k, cut)
-                load_v(k + 5)
 
         with tc.tile_pool(name="early", bufs=1) as early, tc.psum_pool(name="ps_early", bufs=1) as ps_early:
             a_rows = early.tile([P, HEADS * P], BF16)
             nc.sync.dma_start(out=a_rows, in_=a_heads.rearrange("p n i -> p (n i)"))
+            for k in range(V_FIRST):
+                load_v(k)
             s_raw = early.tile([P, P, P], BF16)
             for rc in range(8):
                 r_cols = slice(16 * rc, 16 * rc + 16)
                 nc.sync.dma_start(out=s_raw[:, r_cols, :], in_=step2[r_cols].rearrange("r i q -> i r q"))
-            for k in range(2):
-                load_v(k)
-            nc.sync.dma_start(out=w_rows, in_=W_out.rearrange("(c o) k -> o c k", o=P))
-            for k in range(2, 5):
+            for k in range(V_FIRST, V_RAW):
                 load_v(k)
 
             a_ps = ps_early.tile([P, HEADS, P], BF16)
@@ -170,14 +169,22 @@ def tile_trittentioncube_pb_kernel(tc, a_heads, step2, v_pairs, W_out, b_out, ou
                 nc.tensor.transpose(a_ps[:, n, :], a_rows[:, n * P : (n + 1) * P], ident_bf)
             nc.vector.tensor_copy(out=a_t, in_=a_ps)
 
-            cut = 80
+            cut = 20
             for rc in range(8):
                 r_cols = slice(16 * rc, 16 * rc + 16)
-                src = s_raw[:, r_cols, :].rearrange("i r q -> i q r")
-                nc.vector.tensor_copy(out=s2[:, 0:cut, r_cols], in_=src[:, 0:cut, :])
-                nc.scalar.copy(out=s2[:, cut:P, r_cols], in_=src[:, cut:P, :])
+                src = s_raw[:, r_cols, :].rearrange("i r (c q) -> i c r q", q=4)
+                dst = s2[:, :, r_cols].rearrange("i (c q) r -> i c r q", q=4)
+                nc.vector.tensor_copy(out=dst[:, 0:cut], in_=src[:, 0:cut])
+                nc.scalar.copy(out=dst[:, cut : P // 4], in_=src[:, cut : P // 4])
+                if rc % 2 == 1 and rc // 2 < V_FIRST:
+                    k = rc // 2
+                    group_tile(k)
+                    regroup_by_copy(k, 0, 64, nc.vector.tensor_copy)
+                    regroup_by_copy(k, 64, P, nc.scalar.copy)
+                if rc % 2 == 0 and 0 < rc // 2 <= V_FIRST:
+                    quantise_v(rc // 2 - 1)
 
-        kept = stack.enter_context(tc.tile_pool(name="kept", bufs=4))
+        kept = stack.enter_context(tc.tile_pool(name="kept", bufs=5))
         ps_s = stack.enter_context(tc.psum_pool(name="ps_s", bufs=3))
         ps_t = stack.enter_context(tc.psum_pool(name="ps_t", bufs=2))
         ps_v = stack.enter_context(tc.psum_pool(name="ps_v", bufs=2))
@@ -219,31 +226,28 @@ def tile_trittentioncube_pb_kernel(tc, a_heads, step2, v_pairs, W_out, b_out, ou
                         op1=ALU.max,
                         accum_out=part_max[:, n, QUADS * k + g : QUADS * k + g + 1],
                     )
-            if k == LIVE - 2:
-                nc.vector.tensor_tensor(
-                    out=diag_s[:, n],
-                    in0=diag_s[:, n],
-                    in1=floor.unsqueeze(1).to_broadcast([P, 8, 64]),
-                    op=ALU.max,
-                )
-                nc.vector.tensor_reduce(
-                    out=part_max[:, n, passes : passes + 1],
-                    in_=diag_s[:, n].rearrange("r s x -> r (s x)"),
-                    axis=AX.X,
-                    op=ALU.max,
-                )
-            if k >= LIVE - 2:
-                half = k - LIVE + 2
-                first = half * (UNIT + 128)
-                nc.vector.tensor_copy(
-                    out=d_kept[n % 2][:, first : first + QUADS * (PASS + 32)]
-                    .rearrange("r (g y) -> r g y", g=QUADS)[:, :, 0:PASS]
-                    .rearrange("r g (u x) -> r g u x", u=2)[:, :, :, 0:32],
-                    in_=diag_s[:, n, QUADS * half : QUADS * (half + 1), :].rearrange("r g (u x) -> r g u x", u=2),
-                )
+
+        def diagonal_of(n):
+            nc.gpsimd.tensor_tensor(
+                out=diag_s[:, n], in0=diag_s[:, n], in1=live.unsqueeze(1).to_broadcast([P, 8, 64]), op=ALU.mult
+            )
+            nc.gpsimd.tensor_tensor(
+                out=d_kept[n % 2]
+                .rearrange("r (g y) -> r g y", g=8)[:, :, 0:PASS]
+                .rearrange("r g (u x) -> r g u x", u=2)[:, :, :, 0:32],
+                in0=diag_s[:, n].rearrange("r g (u x) -> r g u x", u=2),
+                in1=dead.rearrange("r (u x) -> r u x", u=2).unsqueeze(1).to_broadcast([P, 8, 2, 32]),
+                op=ALU.add,
+            )
 
         def maximum_of(n):
             one = slice(n, n + 1)
+            nc.vector.tensor_reduce(
+                out=part_max[:, n, passes : passes + 1],
+                in_=diag_s[:, n].rearrange("r s x -> r (s x)"),
+                axis=AX.X,
+                op=ALU.max,
+            )
             nc.vector.tensor_reduce(out=top[:, one], in_=part_max[:, n, :], axis=AX.X, op=ALU.max)
             nc.vector.tensor_scalar(out=neg_m[:, one], in0=top[:, one], scalar1=-INV_DH, scalar2=None, op0=ALU.mult)
 
@@ -274,7 +278,7 @@ def tile_trittentioncube_pb_kernel(tc, a_heads, step2, v_pairs, W_out, b_out, ou
                 accum_out=sums[:, n, k : k + 1],
             )
 
-        def transpose_rows(words, count, copy):
+        def transpose_rows(words, count, shared):
             grouped = e_pool.tile([P, UNIT], BF16, align_bytes=64, name="e_grouped")
             grouped_words = grouped.bitcast(F32).rearrange("x (g r u) -> x g r u", g=QUADS, u=2)
             for first in range(0, count, 2):
@@ -284,6 +288,7 @@ def tile_trittentioncube_pb_kernel(tc, a_heads, step2, v_pairs, W_out, b_out, ou
                     for u in range(2):
                         start_word = 256 * (first + g) + P * u
                         nc.tensor.transpose(t_ps[:, g, u, :], words[:, start_word : start_word + P], ident_f32)
+                copy = nc.vector.tensor_copy if shared and first > 0 else nc.scalar.copy
                 copy(out=grouped_words[:, first : first + pair], in_=t_ps[:, 0:pair].rearrange("x g u r -> x g r u"))
             return grouped
 
@@ -361,29 +366,39 @@ def tile_trittentioncube_pb_kernel(tc, a_heads, step2, v_pairs, W_out, b_out, ou
                             start=True,
                             stop=True,
                         )
-            nc.vector.tensor_tensor(
-                out=diag_s[:, :, 2 * bank : 2 * bank + 2, :],
-                in0=d_ps.rearrange("r (n s x) -> r n s x", n=HEADS, s=2),
-                in1=ceiling.unsqueeze(1).unsqueeze(1).to_broadcast([P, HEADS, 2, 64]),
-                op=ALU.min,
+            nc.scalar.copy(
+                out=diag_s[:, :, 2 * bank : 2 * bank + 2, :].rearrange("r n s x -> r n (s x)"),
+                in_=d_ps.rearrange("r (n x) -> r n x", n=HEADS),
             )
+        for n in range(2):
+            diagonal_of(n)
 
+        for v in range(V_FIRST):
+            load_v(v + V_RAW)
         for k in range(LIVE):
             scores_and_maximum(0, k)
-            regroup_v(k, 0)
-            load_v(k + 5)
+            v = V_FIRST + k
+            group_tile(v)
+            regroup_by_copy(v, 0, P, nc.scalar.copy)
+            load_v(v + V_RAW)
         maximum_of(0)
-        next_v = LIVE
-        for k in range(LIVE - 1):
-            quantise_v(k)
+        next_v = V_FIRST + LIVE
+        scores_and_maximum(1, 0)
+        for v in range(V_FIRST, next_v - 1):
+            quantise_v(v)
 
         units = [(n, k) for n in range(HEADS) for k in range(LIVE)]
         for i in range(len(units) + 3):
+            if 0 <= i - 4 and units[i - 4][1] == LIVE - 1:
+                finish_head(units[i - 4][0])
             if i < len(units):
                 n, k = units[i]
                 if k == 0:
                     exp_const(n)
                 exp_stage(n, k)
+            v_now = range(next_v, max(next_v, min(len(v_order), V_FIRST + LIVE + (i + 1) * V_NUM // V_DEN)))
+            next_v += len(v_now)
+            cut = CUT_LAST if i >= len(units) - LIVE else CUT
             if 0 <= i - 2 < len(units):
                 n, k = units[i - 2]
                 if k == 0:
@@ -395,21 +410,32 @@ def tile_trittentioncube_pb_kernel(tc, a_heads, step2, v_pairs, W_out, b_out, ou
                 n, k = units[i - 1]
                 if k == 0:
                     e_grouped[n, -1] = transpose_const(n)
-                e_grouped[n, k] = transpose_rows(e_rows[n, k].bitcast(F32), QUADS, nc.scalar.copy)
-            if i + LIVE < len(units):
-                n, k = units[i + LIVE]
+                e_grouped[n, k] = transpose_rows(e_rows[n, k].bitcast(F32), QUADS, SHARED and n == HEADS - 1)
+            for v in v_now:
+                group_tile(v)
+                if cut < P:
+                    regroup_by_pe(v, cut)
+            if 0 <= i - 3:
+                multiply_stage(*units[i - 3])
+            if i + LIVE + 1 < len(units):
+                n, k = units[i + LIVE + 1]
                 scores_and_maximum(n, k)
                 if k == LIVE - 1:
                     maximum_of(n)
-            for step in range(2 if i % 5 in (0, 2, 4) else 1):
-                step_v(next_v, P if i >= len(units) - LIVE else 64)
-                next_v += 1
-            if 0 <= i - 4 and units[i - 4][1] == LIVE - 1:
-                finish_head(units[i - 4][0])
-            if 0 <= i - 3:
-                multiply_stage(*units[i - 3])
-            if i == 1:
+            if i % LIVE == LIVE - 1 and i // LIVE + 2 < HEADS:
+                diagonal_of(i // LIVE + 2)
+            for v in v_now:
+                quantise_v(v - 1)
+                regroup_by_copy(v, 0, cut, nc.vector.tensor_copy)
+                load_v(v + V_RAW)
+                if v == len(v_order) - 1:
+                    quantise_v(v)
+            if i == 0:
+                w_rows = stream.tile([P, 4, 512], BF16, name="w_rows", bufs=1)
+                nc.sync.dma_start(out=w_rows, in_=W_out.rearrange("(c o) k -> o c k", o=P))
+            if i == W_ROUND:
                 w_words = w_rows.bitcast(F32)
+                w_grouped = e_pool.tile([P, UNIT], BF16, align_bytes=64, name="e_grouped")
                 w_grouped_words = w_grouped.bitcast(F32).rearrange("x (c o u) -> x c o u", c=4, u=2)
                 for half in range(2):
                     w_ps = ps_t.tile([P, 2, 2, P], F32, name="t_ps")
@@ -419,12 +445,11 @@ def tile_trittentioncube_pb_kernel(tc, a_heads, step2, v_pairs, W_out, b_out, ou
                     nc.vector.tensor_copy(
                         out=w_grouped_words[:, 2 * half : 2 * half + 2], in_=w_ps.rearrange("x c u o -> x c o u")
                     )
-            if i == 2:
                 nc.vector.quantize_mx(out=w_codes.bitcast(FP8X4), scales=w_scales, in_=w_grouped)
                 nc.sync.dma_start(out=bias_rows, in_=b_out.partition_broadcast(P))
 
         finish_head(HEADS - 1)
-        z_codes, z_scales = quantise_rows(transpose_rows(z_bf.bitcast(F32), 1, nc.scalar.copy), 1)
+        z_codes, z_scales = quantise_rows(transpose_rows(z_bf.bitcast(F32), 1, False), 1)
         o_ps = ps_s.tile([P, 512], F32, name="s_ps")
         nc.tensor.matmul_mx(
             out=o_ps,

@@ -40,7 +40,7 @@ V_FIRST = 2
 V_NUM, V_DEN = 5, 4
 W_ROUND = 14
 SHARED = False
-CUT, CUT_LAST = 64, P
+CUT, CUT_LAST = 80, P
 CONST = 256
 
 FLOPS = 2 * 128 * 512 * 128 * 128 + 2 * 4 * 128 * 16384 * 128 + 2 * 128 * 512 * 512
@@ -122,23 +122,6 @@ def tile_trittentioncube_pb_kernel(tc, a_heads, step2, v_pairs, W_out, b_out, ou
                     in_=v_raw[k][:, :, first:last].rearrange("x (g t) (c i) -> x g c t i", t=4, i=4),
                 )
 
-        def regroup_by_pe(k, first):
-            for half in range(2):
-                v_ps = ps_v.tile([P, 2, P - first, 4], BF16, name="v_ps")
-                for g in range(2):
-                    t_rows = slice(8 * half + 4 * g, 8 * half + 4 * g + 4)
-                    nc.tensor.matmul(
-                        out=v_ps[:, g],
-                        lhsT=ident_bf,
-                        rhs=v_raw[k][:, t_rows, first:P].rearrange("x t f -> x f t"),
-                        start=True,
-                        stop=True,
-                    )
-                nc.scalar.copy(
-                    out=v_grouped[k][:, 2 * half : 2 * half + 2, first:P].rearrange("x g f t -> x g (f t)"),
-                    in_=v_ps.rearrange("x g f t -> x g (f t)"),
-                )
-
         def group_tile(k):
             v_grouped[k] = stream.tile([P, QUADS, P, 4], BF16, align_bytes=64, name="v_grouped", bufs=5)
 
@@ -186,9 +169,8 @@ def tile_trittentioncube_pb_kernel(tc, a_heads, step2, v_pairs, W_out, b_out, ou
 
         kept = stack.enter_context(tc.tile_pool(name="kept", bufs=5))
         ps_s = stack.enter_context(tc.psum_pool(name="ps_s", bufs=3))
-        ps_t = stack.enter_context(tc.psum_pool(name="ps_t", bufs=2))
-        ps_v = stack.enter_context(tc.psum_pool(name="ps_v", bufs=2))
-        ps_z = stack.enter_context(tc.psum_pool(name="ps_z", bufs=1))
+        ps_t = stack.enter_context(tc.psum_pool(name="ps_t", bufs=3))
+        ps_z = stack.enter_context(tc.psum_pool(name="ps_z", bufs=2))
 
         s_kept = {}
 
@@ -413,8 +395,7 @@ def tile_trittentioncube_pb_kernel(tc, a_heads, step2, v_pairs, W_out, b_out, ou
                 e_grouped[n, k] = transpose_rows(e_rows[n, k].bitcast(F32), QUADS, SHARED and n == HEADS - 1)
             for v in v_now:
                 group_tile(v)
-                if cut < P:
-                    regroup_by_pe(v, cut)
+                regroup_by_copy(v, cut, P, nc.scalar.copy)
             if 0 <= i - 3:
                 multiply_stage(*units[i - 3])
             if i + LIVE + 1 < len(units):

@@ -25,39 +25,46 @@ UNIT = QUADS * PASS
 FULL_A = ((0, 64), (32, 64), (0, 32), (64, 96))
 FULL_B = ((0, 80), (32, 80), (0, 48), (64, 112))
 FULL_C = ((0, 96), (32, 96), (0, 112), (32, 112))
-DIAG_A = ((0, 0), (32, 32), (64, 64), (96, 96))
 DIAG_B = ((0, 16), (32, 48), (64, 80), (96, 112))
 MASK_A = ((64, 0), (96, 0), (32, 0), (96, 64))
 MASK_B = ((64, 16), (96, 16), (32, 16), (96, 80))
 MASK_C = ((64, 32), (96, 32), (64, 48), (96, 48))
+DIAG_A = ((0, 0), (32, 32), (64, 64), (96, 96))
+FOLD_ROWS, FOLD_SLOTS = 16, 8
+
 LIVE_UNITS = (FULL_A, FULL_B, FULL_C, DIAG_A, DIAG_B)
-MASK_UNITS = (MASK_A, MASK_B, MASK_C)
-V_UNITS = MASK_UNITS + LIVE_UNITS
+V_UNITS = (MASK_A, MASK_B, MASK_C) + LIVE_UNITS
+MASKS = 3
 LIVE = len(LIVE_UNITS)
-MASKED_PAIRS = len(MASK_UNITS) * UNIT
+FOLDED = LIVE_UNITS.index(DIAG_A)
+LIVE_PASSES = (4, 4, 4, 2, 4)
+MASKED_PAIRS = (4 * MASKS + 2) * PASS
 V_RAW = 5
 V_FIRST = 2
 V_NUM, V_DEN = 5, 4
 W_ROUND = 14
 SHARED = False
-CUT, CUT_LAST = 80, P
+CUT, CUT_LAST = 40, P
+GP = 48
 CONST = 256
 
 FLOPS = 2 * 128 * 512 * 128 * 128 + 2 * 4 * 128 * 16384 * 128 + 2 * 128 * 512 * 512
 
 
-def live_rows(k, g):
+def live_parts(k, g):
+    corners = [(p0, q0 + 4 * g) for p0, q0 in LIVE_UNITS[k]]
     if LIVE_UNITS[k] == DIAG_A:
-        return 4 * g
+        later = [(p0, q0 + FOLD_SLOTS) for p0, q0 in corners]
+        return [(0, 4 * g, corners), (FOLD_ROWS, FOLD_SLOTS + 4 * g, later)]
     if LIVE_UNITS[k] == DIAG_B:
-        return SLOTS + 4 * g
-    return ROWS
+        return [(0, SLOTS + 4 * g, corners)]
+    return [(0, ROWS, corners)]
 
 
 def tile_trittentioncube_pb_kernel(tc, a_heads, step2, v_pairs, W_out, b_out, out):
     nc = tc.nc
     v_plane = v_pairs.rearrange("n (p q) f -> n p q f", q=P)
-    passes = LIVE * QUADS
+    diag_col = 4 * LIVE
 
     with ExitStack() as stack:
         stack.enter_context(tc.manual_schedule())
@@ -71,8 +78,8 @@ def tile_trittentioncube_pb_kernel(tc, a_heads, step2, v_pairs, W_out, b_out, ou
         w_codes = keep.tile([P, 512], U32, align_bytes=64)
         w_scales = keep.tile([P, 512], U8, align_bytes=64)
         bias_rows = keep.tile([P, 512], BF16)
-        d_kept = [keep.tile([P, 2 * UNIT + 8 * 32], F32, name="d_kept%d" % k) for k in range(2)]
-        part_max = keep.tile([P, HEADS, passes + 1], F32)
+        d_kept = [keep.tile([P, 6 * PASS + 8 * 32], F32, name="d_kept%d" % k) for k in range(2)]
+        part_max = keep.tile([P, HEADS, diag_col + 1], F32)
         sums = keep.tile([P, HEADS, LIVE + 1], F32)
         top = keep.tile([P, HEADS], F32)
         neg_m = keep.tile([P, HEADS], F32)
@@ -80,6 +87,7 @@ def tile_trittentioncube_pb_kernel(tc, a_heads, step2, v_pairs, W_out, b_out, ou
         recip = keep.tile([P, HEADS], F32)
         fill_col = keep.tile([P, 1], F32)
         warm = keep.tile([P, 1], F32)
+        go = keep.tile([P, HEADS * LIVE], F32)
         live = keep.tile([P, 64], F32)
         dead = keep.tile([P, 64], F32)
         diag_s = keep.tile([P, HEADS, 8, 64], F32)
@@ -113,7 +121,17 @@ def tile_trittentioncube_pb_kernel(tc, a_heads, step2, v_pairs, W_out, b_out, ou
                 n, j = v_order[k]
                 v_raw[k] = stream.tile([P, SLOTS, P], BF16, name="v_raw", bufs=V_RAW)
                 for b, (p0, q0) in enumerate(V_UNITS[j]):
-                    nc.sync.dma_start(out=v_raw[k][b:P:4, :, :], in_=v_plane[n, p0 : p0 + ROWS, q0 : q0 + SLOTS, :])
+                    if V_UNITS[j] == DIAG_A:
+                        for fold in range(2):
+                            q1 = q0 + FOLD_SLOTS * fold
+                            for part in range(2):
+                                p1 = p0 + FOLD_ROWS * part
+                                nc.sync.dma_start(
+                                    out=v_raw[k][64 * fold + b : 64 * fold + 64 : 4, FOLD_SLOTS * part : FOLD_SLOTS * (part + 1), :],
+                                    in_=v_plane[n, p1 : p1 + FOLD_ROWS, q1 : q1 + FOLD_SLOTS, :],
+                                )
+                    else:
+                        nc.sync.dma_start(out=v_raw[k][b:P:4, :, :], in_=v_plane[n, p0 : p0 + ROWS, q0 : q0 + SLOTS, :])
 
         def regroup_by_copy(k, first, last, copy):
             if first < last:
@@ -175,57 +193,62 @@ def tile_trittentioncube_pb_kernel(tc, a_heads, step2, v_pairs, W_out, b_out, ou
         s_kept = {}
 
         def scores_and_maximum(n, k):
-            corners = LIVE_UNITS[k]
-            if k < LIVE - 2:
+            if k < FOLDED:
                 s_kept[n, k] = kept.tile([P, UNIT], F32, name="s_kept")
+            elif k == FOLDED:
+                s_kept[n, k] = d_kept[n % 2][:, 0 : 2 * PASS]
             else:
-                s_kept[n, k] = d_kept[n % 2][:, (k - LIVE + 2) * UNIT : (k - LIVE + 3) * UNIT]
-            for g in range(QUADS):
-                rows = live_rows(k, g)
-                if rows > 0:
-                    s_ps = ps_s.tile([P, PASS], F32, name="s_ps")
-                    cells = s_ps.rearrange("r (u b e i) -> r u b e i", u=2, b=4, e=2)
-                    for t in range(4):
-                        b = 0
-                        while b < 4:
-                            p0, q0 = corners[b]
-                            wide = 2 if rows == ROWS and b < 3 and corners[b + 1] == (p0 + ROWS, q0) else 1
-                            nc.tensor.matmul(
-                                out=cells[:, t // 2, b : b + wide, t % 2, 0:rows],
-                                lhsT=s2[:, q0 + 4 * g + t, :],
-                                rhs=a_t[:, n, p0 : p0 + wide * rows].rearrange("i (b p) -> i b p", b=wide),
-                                start=True,
-                                stop=True,
-                            )
-                            b += wide
-                    nc.vector.tensor_scalar(
-                        out=s_kept[n, k][:, g * PASS : (g + 1) * PASS]
-                        .rearrange("r (u i c) -> r u i c", u=2, c=8)[:, :, 0:rows, :],
-                        in0=s_ps.rearrange("r (u c i) -> r u i c", u=2, c=8)[:, :, 0:rows, :],
-                        scalar1=1.0,
-                        scalar2=None,
-                        op0=ALU.mult,
-                        op1=ALU.max,
-                        accum_out=part_max[:, n, QUADS * k + g : QUADS * k + g + 1],
-                    )
+                s_kept[n, k] = d_kept[n % 2][:, 2 * PASS : 6 * PASS]
+            for g in range(LIVE_PASSES[k]):
+                s_ps = ps_s.tile([P, PASS], F32, name="s_ps")
+                cells = s_ps.rearrange("r (u b e i) -> r u b e i", u=2, b=4, e=2)
+                for part, (i0, rows, corners) in enumerate(live_parts(k, g)):
+                    if rows > 0:
+                        for t in range(4):
+                            b = 0
+                            while b < 4:
+                                p0, q0 = corners[b]
+                                wide = 2 if rows == ROWS and b < 3 and corners[b + 1] == (p0 + ROWS, q0) else 1
+                                nc.tensor.matmul(
+                                    out=cells[:, t // 2, b : b + wide, t % 2, i0 : i0 + rows],
+                                    lhsT=s2[:, q0 + t, :],
+                                    rhs=a_t[:, n, p0 : p0 + wide * rows].rearrange("i (b p) -> i b p", b=wide),
+                                    start=True,
+                                    stop=True,
+                                )
+                                b += wide
+                for part, (i0, rows, corners) in enumerate(live_parts(k, g)):
+                    if rows > 0:
+                        column = 4 * k + 2 * part + g
+                        nc.vector.tensor_scalar(
+                            out=s_kept[n, k][:, g * PASS : (g + 1) * PASS]
+                            .rearrange("r (u i c) -> r u i c", u=2, c=8)[:, :, i0 : i0 + rows, :],
+                            in0=s_ps.rearrange("r (u c i) -> r u i c", u=2, c=8)[:, :, i0 : i0 + rows, :],
+                            scalar1=1.0,
+                            scalar2=None,
+                            op0=ALU.mult,
+                            op1=ALU.max,
+                            accum_out=part_max[:, n, column : column + 1],
+                        )
 
         def diagonal_of(n):
             nc.gpsimd.tensor_tensor(
                 out=diag_s[:, n], in0=diag_s[:, n], in1=live.unsqueeze(1).to_broadcast([P, 8, 64]), op=ALU.mult
             )
-            nc.gpsimd.tensor_tensor(
-                out=d_kept[n % 2]
-                .rearrange("r (g y) -> r g y", g=8)[:, :, 0:PASS]
-                .rearrange("r g (u x) -> r g u x", u=2)[:, :, :, 0:32],
-                in0=diag_s[:, n].rearrange("r g (u x) -> r g u x", u=2),
-                in1=dead.rearrange("r (u x) -> r u x", u=2).unsqueeze(1).to_broadcast([P, 8, 2, 32]),
-                op=ALU.add,
-            )
+            for j, count, first in ((0, 2, 0), (2, 2, 128 + 64), (4, 4, 2 * PASS + 128)):
+                nc.gpsimd.tensor_tensor(
+                    out=d_kept[n % 2][:, first : first + count * (PASS + 32)]
+                    .rearrange("r (g y) -> r g y", g=count)[:, :, 0:PASS]
+                    .rearrange("r g (u x) -> r g u x", u=2)[:, :, :, 0:32],
+                    in0=diag_s[:, n, j : j + count].rearrange("r g (u x) -> r g u x", u=2),
+                    in1=dead.rearrange("r (u x) -> r u x", u=2).unsqueeze(1).to_broadcast([P, count, 2, 32]),
+                    op=ALU.add,
+                )
 
         def maximum_of(n):
             one = slice(n, n + 1)
             nc.vector.tensor_reduce(
-                out=part_max[:, n, passes : passes + 1],
+                out=part_max[:, n, diag_col : diag_col + 1],
                 in_=diag_s[:, n].rearrange("r s x -> r (s x)"),
                 axis=AX.X,
                 op=ALU.max,
@@ -252,7 +275,7 @@ def tile_trittentioncube_pb_kernel(tc, a_heads, step2, v_pairs, W_out, b_out, ou
         def exp_stage(n, k):
             e_rows[n, k] = e_pool.tile([P, UNIT], BF16, name="e_rows")
             nc.scalar.activation(
-                out=e_rows[n, k],
+                out=e_rows[n, k][:, 0 : LIVE_PASSES[k] * PASS],
                 in_=s_kept[n, k],
                 func=ACT.Exp,
                 bias=neg_m[:, n : n + 1],
@@ -295,9 +318,11 @@ def tile_trittentioncube_pb_kernel(tc, a_heads, step2, v_pairs, W_out, b_out, ou
             return codes, scales
 
         def quantise_const(grouped):
-            codes = e_pool.tile([P, P], U32, align_bytes=64, name="e_const_codes", bufs=2)
-            scales = e_pool.tile([P, P], U8, align_bytes=64, name="e_const_scales", bufs=2)
-            nc.vector.quantize_mx(out=codes.bitcast(FP8X4), scales=scales, in_=grouped)
+            codes = e_pool.tile([P, 2 * P], U32, align_bytes=64, name="e_const_codes", bufs=2)
+            scales = e_pool.tile([P, 2 * P], U8, align_bytes=64, name="e_const_scales", bufs=2)
+            for copy in range(2):
+                cols = slice(copy * P, (copy + 1) * P)
+                nc.vector.quantize_mx(out=codes[:, cols].bitcast(FP8X4), scales=scales[:, cols], in_=grouped)
             return codes, scales
 
         def add_pass(n, e_pair, g, v_pair, h, first, last):
@@ -314,11 +339,14 @@ def tile_trittentioncube_pb_kernel(tc, a_heads, step2, v_pairs, W_out, b_out, ou
         def multiply_stage(n, k):
             if k == 0:
                 z_ps[n] = ps_z.tile([P, P], F32, name="z_ps")
-                for j in range(len(MASK_UNITS)):
+                for j in range(MASKS):
                     for h in range(QUADS):
-                        add_pass(n, e_codes[n, -1], 0, v_codes[n, j], h, j == 0 and h == 0, False)
+                        add_pass(n, e_codes[n, -1], h % 2, v_codes[n, j], h, j == 0 and h == 0, False)
             for g in range(QUADS):
-                add_pass(n, e_codes[n, k], g, v_codes[n, len(MASK_UNITS) + k], g, False, k == LIVE - 1 and g == QUADS - 1)
+                if g < LIVE_PASSES[k]:
+                    add_pass(n, e_codes[n, k], g, v_codes[n, MASKS + k], g, False, k == LIVE - 1 and g == QUADS - 1)
+                else:
+                    add_pass(n, e_codes[n, -1], g % 2, v_codes[n, MASKS + k], g, False, False)
 
         def divisor_of(n):
             one = slice(n, n + 1)
@@ -380,25 +408,37 @@ def tile_trittentioncube_pb_kernel(tc, a_heads, step2, v_pairs, W_out, b_out, ou
                 exp_stage(n, k)
             v_now = range(next_v, max(next_v, min(len(v_order), V_FIRST + LIVE + (i + 1) * V_NUM // V_DEN)))
             next_v += len(v_now)
+            gp = GP if i + LIVE + 1 < len(units) else 0
             cut = CUT_LAST if i >= len(units) - LIVE else CUT
             if 0 <= i - 2 < len(units):
                 n, k = units[i - 2]
                 if k == 0:
                     e_codes[n, -1] = quantise_const(e_grouped[n, -1])
-                e_codes[n, k] = quantise_rows(e_grouped[n, k], QUADS)
+                e_codes[n, k] = quantise_rows(e_grouped[n, k], LIVE_PASSES[k])
                 if k == LIVE - 1:
                     divisor_of(n)
             if 0 <= i - 1 < len(units):
                 n, k = units[i - 1]
                 if k == 0:
                     e_grouped[n, -1] = transpose_const(n)
-                e_grouped[n, k] = transpose_rows(e_rows[n, k].bitcast(F32), QUADS, SHARED and n == HEADS - 1)
+                e_grouped[n, k] = transpose_rows(e_rows[n, k].bitcast(F32), LIVE_PASSES[k], SHARED and n == HEADS - 1)
             for v in v_now:
                 group_tile(v)
-                regroup_by_copy(v, cut, P, nc.scalar.copy)
+                regroup_by_copy(v, cut, P - gp, nc.scalar.copy)
             if 0 <= i - 3:
                 multiply_stage(*units[i - 3])
             if i + LIVE + 1 < len(units):
+                if gp > 0 and len(v_now) > 0:
+                    nc.vector.memset(go[:, i : i + 1], 1.0)
+                    for v in v_now:
+                        nc.gpsimd.tensor_scalar(
+                            out=v_grouped[v][:, :, P - gp : P, :],
+                            in0=v_raw[v][:, :, P - gp : P].rearrange("x (g t) f -> x g f t", t=4),
+                            scalar1=go[:, i : i + 1],
+                            scalar2=0.0,
+                            op0=ALU.mult,
+                            op1=ALU.add,
+                        )
                 n, k = units[i + LIVE + 1]
                 scores_and_maximum(n, k)
                 if k == LIVE - 1:

@@ -41,11 +41,12 @@ LIVE_PASSES = (4, 4, 4, 2, 4)
 MASKED_PAIRS = (4 * MASKS + 2) * PASS
 V_RAW = 5
 V_FIRST = 2
-V_NUM, V_DEN = 5, 4
+V_NUM, V_DEN = 4, 3
 W_ROUND = 14
 SHARED = False
-CUT, CUT_LAST = 40, P
-GP = 48
+CUT, CUT_LAST = 48, P
+WARM_PIECES, WARM_MATMULS = 3, 3
+GP = 32
 CONST = 256
 
 FLOPS = 2 * 128 * 512 * 128 * 128 + 2 * 4 * 128 * 16384 * 128 + 2 * 128 * 512 * 512
@@ -166,6 +167,7 @@ def tile_trittentioncube_pb_kernel(tc, a_heads, step2, v_pairs, W_out, b_out, ou
                 load_v(k)
 
             a_ps = ps_early.tile([P, HEADS, P], BF16)
+            w_bank = ps_early.tile([P, 32, 16], F32)
             for n in range(HEADS):
                 nc.tensor.transpose(a_ps[:, n, :], a_rows[:, n * P : (n + 1) * P], ident_bf)
             nc.vector.tensor_copy(out=a_t, in_=a_ps)
@@ -177,6 +179,11 @@ def tile_trittentioncube_pb_kernel(tc, a_heads, step2, v_pairs, W_out, b_out, ou
                 dst = s2[:, :, r_cols].rearrange("i (c q) r -> i c r q", q=4)
                 nc.vector.tensor_copy(out=dst[:, 0:cut], in_=src[:, 0:cut])
                 nc.scalar.copy(out=dst[:, cut : P // 4], in_=src[:, cut : P // 4])
+                if rc >= 8 - WARM_PIECES:
+                    for turn in range(WARM_MATMULS):
+                        nc.tensor.matmul(
+                            out=w_bank, lhsT=ident_bf, rhs=s2[:, 0:32, r_cols], start=True, stop=True
+                        )
                 if rc % 2 == 1 and rc // 2 < V_FIRST:
                     k = rc // 2
                     group_tile(k)
@@ -186,9 +193,9 @@ def tile_trittentioncube_pb_kernel(tc, a_heads, step2, v_pairs, W_out, b_out, ou
                     quantise_v(rc // 2 - 1)
 
         kept = stack.enter_context(tc.tile_pool(name="kept", bufs=5))
-        ps_s = stack.enter_context(tc.psum_pool(name="ps_s", bufs=3))
+        ps_s = stack.enter_context(tc.psum_pool(name="ps_s", bufs=4))
         ps_t = stack.enter_context(tc.psum_pool(name="ps_t", bufs=3))
-        ps_z = stack.enter_context(tc.psum_pool(name="ps_z", bufs=2))
+        ps_z = stack.enter_context(tc.psum_pool(name="ps_z", bufs=1))
 
         s_kept = {}
 

@@ -41,13 +41,14 @@ LIVE_PASSES = (4, 4, 4, 2, 4)
 MASKED_PAIRS = (4 * MASKS + 2) * PASS
 V_RAW = 5
 V_FIRST = 2
+V_NEXT = 4
 V_NUM, V_DEN = 4, 3
 W_ROUND = 14
 SHARED = False
-CUT, CUT_LAST = 48, P
+CUT, CUT_LAST = 56, P
 WARM_PIECES, WARM_MATMULS = 3, 3
 GP = 32
-CONST = 256
+CONST = 2
 
 FLOPS = 2 * 128 * 512 * 128 * 128 + 2 * 4 * 128 * 16384 * 128 + 2 * 128 * 512 * 512
 
@@ -82,6 +83,7 @@ def tile_trittentioncube_pb_kernel(tc, a_heads, step2, v_pairs, W_out, b_out, ou
         d_kept = [keep.tile([P, 6 * PASS + 8 * 32], F32, name="d_kept%d" % k) for k in range(2)]
         part_max = keep.tile([P, HEADS, diag_col + 1], F32)
         sums = keep.tile([P, HEADS, LIVE + 1], F32)
+        const_sum = keep.tile([P, HEADS], F32)
         top = keep.tile([P, HEADS], F32)
         neg_m = keep.tile([P, HEADS], F32)
         total = keep.tile([P, HEADS], F32)
@@ -206,6 +208,8 @@ def tile_trittentioncube_pb_kernel(tc, a_heads, step2, v_pairs, W_out, b_out, ou
                 s_kept[n, k] = d_kept[n % 2][:, 0 : 2 * PASS]
             else:
                 s_kept[n, k] = d_kept[n % 2][:, 2 * PASS : 6 * PASS]
+            if k == FOLDED:
+                diagonal_maximum(n)
             for g in range(LIVE_PASSES[k]):
                 s_ps = ps_s.tile([P, PASS], F32, name="s_ps")
                 cells = s_ps.rearrange("r (u b e i) -> r u b e i", u=2, b=4, e=2)
@@ -252,16 +256,20 @@ def tile_trittentioncube_pb_kernel(tc, a_heads, step2, v_pairs, W_out, b_out, ou
                     op=ALU.add,
                 )
 
-        def maximum_of(n):
-            one = slice(n, n + 1)
+        def diagonal_maximum(n):
             nc.vector.tensor_reduce(
                 out=part_max[:, n, diag_col : diag_col + 1],
                 in_=diag_s[:, n].rearrange("r s x -> r (s x)"),
                 axis=AX.X,
                 op=ALU.max,
             )
+
+        def maximum_of(n):
+            one = slice(n, n + 1)
             nc.vector.tensor_reduce(out=top[:, one], in_=part_max[:, n, :], axis=AX.X, op=ALU.max)
-            nc.vector.tensor_scalar(out=neg_m[:, one], in0=top[:, one], scalar1=-INV_DH, scalar2=None, op0=ALU.mult)
+            nc.gpsimd.tensor_scalar(
+                out=neg_m[:, one], in0=top[:, one], scalar1=-INV_DH, scalar2=0.0, op0=ALU.mult, op1=ALU.add
+            )
 
         e_rows = {}
         e_grouped = {}
@@ -276,7 +284,7 @@ def tile_trittentioncube_pb_kernel(tc, a_heads, step2, v_pairs, W_out, b_out, ou
                 func=ACT.Exp,
                 bias=neg_m[:, n : n + 1],
                 scale=INV_DH,
-                accum_out=sums[:, n, LIVE : LIVE + 1],
+                accum_out=const_sum[:, n : n + 1],
             )
 
         def exp_stage(n, k):
@@ -295,7 +303,7 @@ def tile_trittentioncube_pb_kernel(tc, a_heads, step2, v_pairs, W_out, b_out, ou
             grouped_words = grouped.bitcast(F32).rearrange("x (g r u) -> x g r u", g=QUADS, u=2)
             for first in range(0, count, 2):
                 pair = min(2, count - first)
-                t_ps = ps_t.tile([P, 2, 2, P], F32, name="t_ps")
+                t_ps = ps_t.tile([P, PASS], F32, name="t_ps").rearrange("x (g u r) -> x g u r", g=2, u=2)
                 for g in range(pair):
                     for u in range(2):
                         start_word = 256 * (first + g) + P * u
@@ -306,8 +314,8 @@ def tile_trittentioncube_pb_kernel(tc, a_heads, step2, v_pairs, W_out, b_out, ou
 
         def transpose_const(n):
             grouped = e_pool.tile([P, PASS], BF16, align_bytes=64, name="e_const_grouped", bufs=1)
-            t_ps = ps_t.tile([P, 2, 2, P], F32, name="t_ps")
-            nc.tensor.transpose(t_ps[:, 0, 0, :], e_rows[n, -1].bitcast(F32), ident_f32)
+            t_ps = ps_t.tile([P, PASS], F32, name="t_ps").rearrange("x (g u r) -> x g u r", g=2, u=2)
+            nc.tensor.transpose(t_ps[:, 0, 0, :], e_rows[n, -1].bitcast(F32).to_broadcast([P, P]), ident_f32)
             nc.scalar.copy(
                 out=grouped.bitcast(F32).rearrange("x (r u) -> x r u", u=2),
                 in_=t_ps[:, 0, 0, :].unsqueeze(2).to_broadcast([P, P, 2]),
@@ -355,51 +363,54 @@ def tile_trittentioncube_pb_kernel(tc, a_heads, step2, v_pairs, W_out, b_out, ou
                 else:
                     add_pass(n, e_codes[n, -1], g % 2, v_codes[n, MASKS + k], g, False, False)
 
-        def divisor_of(n):
-            one = slice(n, n + 1)
-            nc.vector.tensor_reduce(out=total[:, one], in_=sums[:, n, :], axis=AX.X, op=ALU.add)
-            nc.vector.scalar_tensor_tensor(
-                out=total[:, one], in0=sums[:, n, LIVE : LIVE + 1], scalar=float(MASKED_PAIRS // CONST - 1),
-                in1=total[:, one], op0=ALU.mult, op1=ALU.add,
+        def masked_sum(n):
+            nc.gpsimd.tensor_scalar(
+                out=sums[:, n, LIVE : LIVE + 1],
+                in0=const_sum[:, n : n + 1],
+                scalar1=float(MASKED_PAIRS // CONST),
+                scalar2=0.0,
+                op0=ALU.mult,
+                op1=ALU.add,
             )
-            nc.vector.reciprocal(out=recip[:, one], in_=total[:, one])
 
         def finish_head(n):
             nc.scalar.activation(
                 out=z_bf[:, n * P : (n + 1) * P], in_=z_ps[n], func=ACT.Copy, scale=recip[:, n : n + 1]
             )
 
-        for bank in range(4):
-            d_ps = ps_s.tile([P, PASS], F32, name="s_ps")
-            d_cells = d_ps.rearrange("r (n s u i b e) -> r n s u i b e", n=HEADS, s=2, u=2, i=4, b=4)
-            for s_in in range(2):
-                for b in range(4):
-                    corner = ROWS * b + 4 * (2 * bank + s_in)
-                    for t in range(4):
-                        nc.tensor.matmul(
-                            out=d_cells[:, :, s_in, t // 2, :, b, t % 2],
-                            lhsT=s2[:, corner + t, :],
-                            rhs=a_t[:, :, corner : corner + 4],
-                            start=True,
-                            stop=True,
-                        )
-            nc.scalar.copy(
-                out=diag_s[:, :, 2 * bank : 2 * bank + 2, :].rearrange("r n s x -> r n (s x)"),
-                in_=d_ps.rearrange("r (n x) -> r n x", n=HEADS),
-            )
-        for n in range(2):
-            diagonal_of(n)
-
         for v in range(V_FIRST):
             load_v(v + V_RAW)
         for k in range(LIVE):
             scores_and_maximum(0, k)
-            v = V_FIRST + k
-            group_tile(v)
-            regroup_by_copy(v, 0, P, nc.scalar.copy)
-            load_v(v + V_RAW)
+            if k < V_NEXT:
+                v = V_FIRST + k
+                group_tile(v)
+                regroup_by_copy(v, 0, P, nc.scalar.copy)
+                load_v(v + V_RAW)
+            if k < 2:
+                for bank in range(2 * k, 2 * k + 2):
+                    d_ps = ps_t.tile([P, PASS], F32, name="t_ps")
+                    d_cells = d_ps.rearrange("r (n s u i b e) -> r n s u i b e", n=HEADS, s=2, u=2, i=4, b=4)
+                    for s_in in range(2):
+                        for b in range(4):
+                            corner = ROWS * b + 4 * (2 * bank + s_in)
+                            for t in range(4):
+                                nc.tensor.matmul(
+                                    out=d_cells[:, :, s_in, t // 2, :, b, t % 2],
+                                    lhsT=s2[:, corner + t, :],
+                                    rhs=a_t[:, :, corner : corner + 4],
+                                    start=True,
+                                    stop=True,
+                                )
+                    nc.scalar.copy(
+                        out=diag_s[:, :, 2 * bank : 2 * bank + 2, :].rearrange("r n s x -> r n (s x)"),
+                        in_=d_ps.rearrange("r (n x) -> r n x", n=HEADS),
+                    )
+            if k == 1:
+                for n in range(2):
+                    diagonal_of(n)
         maximum_of(0)
-        next_v = V_FIRST + LIVE
+        next_v = V_FIRST + V_NEXT
         scores_and_maximum(1, 0)
         for v in range(V_FIRST, next_v - 1):
             quantise_v(v)
@@ -413,7 +424,7 @@ def tile_trittentioncube_pb_kernel(tc, a_heads, step2, v_pairs, W_out, b_out, ou
                 if k == 0:
                     exp_const(n)
                 exp_stage(n, k)
-            v_now = range(next_v, max(next_v, min(len(v_order), V_FIRST + LIVE + (i + 1) * V_NUM // V_DEN)))
+            v_now = range(next_v, max(next_v, min(len(v_order), V_FIRST + V_NEXT + (i + 1) * V_NUM // V_DEN)))
             next_v += len(v_now)
             gp = GP if i + LIVE + 1 < len(units) else 0
             cut = CUT_LAST if i >= len(units) - LIVE else CUT
@@ -421,9 +432,14 @@ def tile_trittentioncube_pb_kernel(tc, a_heads, step2, v_pairs, W_out, b_out, ou
                 n, k = units[i - 2]
                 if k == 0:
                     e_codes[n, -1] = quantise_const(e_grouped[n, -1])
+                one = slice(n, n + 1)
+                if k == 1:
+                    masked_sum(n)
+                if k == LIVE - 1:
+                    nc.vector.tensor_reduce(out=total[:, one], in_=sums[:, n, :], axis=AX.X, op=ALU.add)
                 e_codes[n, k] = quantise_rows(e_grouped[n, k], LIVE_PASSES[k])
                 if k == LIVE - 1:
-                    divisor_of(n)
+                    nc.vector.reciprocal(out=recip[:, one], in_=total[:, one])
             if 0 <= i - 1 < len(units):
                 n, k = units[i - 1]
                 if k == 0:
@@ -448,16 +464,16 @@ def tile_trittentioncube_pb_kernel(tc, a_heads, step2, v_pairs, W_out, b_out, ou
                         )
                 n, k = units[i + LIVE + 1]
                 scores_and_maximum(n, k)
-                if k == LIVE - 1:
-                    maximum_of(n)
             if i % LIVE == LIVE - 1 and i // LIVE + 2 < HEADS:
                 diagonal_of(i // LIVE + 2)
             for v in v_now:
-                quantise_v(v - 1)
                 regroup_by_copy(v, 0, cut, nc.vector.tensor_copy)
+                quantise_v(v - 1)
                 load_v(v + V_RAW)
                 if v == len(v_order) - 1:
                     quantise_v(v)
+            if i + LIVE + 1 < len(units) and units[i + LIVE + 1][1] == LIVE - 1:
+                maximum_of(units[i + LIVE + 1][0])
             if i == 0:
                 w_rows = stream.tile([P, 4, 512], BF16, name="w_rows", bufs=1)
                 nc.sync.dma_start(out=w_rows, in_=W_out.rearrange("(c o) k -> o c k", o=P))
@@ -466,7 +482,7 @@ def tile_trittentioncube_pb_kernel(tc, a_heads, step2, v_pairs, W_out, b_out, ou
                 w_grouped = e_pool.tile([P, UNIT], BF16, align_bytes=64, name="e_grouped")
                 w_grouped_words = w_grouped.bitcast(F32).rearrange("x (c o u) -> x c o u", c=4, u=2)
                 for half in range(2):
-                    w_ps = ps_t.tile([P, 2, 2, P], F32, name="t_ps")
+                    w_ps = ps_t.tile([P, PASS], F32, name="t_ps").rearrange("x (g u r) -> x g u r", g=2, u=2)
                     for c in range(2):
                         for u in range(2):
                             nc.tensor.transpose(w_ps[:, c, u, :], w_words[:, 2 * half + c, u * P : (u + 1) * P], ident_f32)

from contextlib import ExitStack

import concourse.mybir as mybir
from concourse.masks import make_identity

F32 = mybir.dt.float32
BF16 = mybir.dt.bfloat16
U32 = mybir.dt.uint32
U8 = mybir.dt.uint8
FP8X4 = mybir.dt.float8_e4m3fn_x4
ALU = mybir.AluOpType
ACT = mybir.ActivationFunctionType
AX = mybir.AxisListType

P = 128
HEADS = 4
FILL = 1e-6
INV_DH = 1.0 / 128.0
ROWS = 32
SLOTS = 16
PASS = 512
QUADS = 4
UNIT = QUADS * PASS

FULL_A = ((0, 64), (32, 64), (0, 32), (64, 96))
FULL_B = ((0, 80), (32, 80), (0, 48), (64, 112))
FULL_C = ((0, 96), (32, 96), (0, 112), (32, 112))
DIAG_B = ((0, 16), (32, 48), (64, 80), (96, 112))
MASK_A = ((64, 0), (96, 0), (32, 0), (96, 64))
MASK_B = ((64, 16), (96, 16), (32, 16), (96, 80))
MASK_C = ((64, 32), (96, 32), (64, 48), (96, 48))
DIAG_A = ((0, 0), (32, 32), (64, 64), (96, 96))
FOLD_ROWS, FOLD_SLOTS = 16, 8

LIVE_UNITS = (FULL_A, FULL_B, FULL_C, DIAG_A, DIAG_B)
V_UNITS = (MASK_A, MASK_B, MASK_C) + LIVE_UNITS
MASKS = 3
LIVE = len(LIVE_UNITS)
FOLDED = LIVE_UNITS.index(DIAG_A)
LIVE_PASSES = (4, 4, 4, 2, 4)
MASKED_PAIRS = (4 * MASKS + 2) * PASS
V_RAW = 5
V_FIRST = 2
V_NEXT = 4
V_NUM, V_DEN = 4, 3
W_ROUND = 14
SHARED = False
CUT, CUT_LAST = 56, P
WARM_PIECES, WARM_MATMULS = 3, 3
GP = 32
CONST = 2

FLOPS = 2 * 128 * 512 * 128 * 128 + 2 * 4 * 128 * 16384 * 128 + 2 * 128 * 512 * 512


def live_parts(k, g):
    corners = [(p0, q0 + 4 * g) for p0, q0 in LIVE_UNITS[k]]
    if LIVE_UNITS[k] == DIAG_A:
        later = [(p0, q0 + FOLD_SLOTS) for p0, q0 in corners]
        return [(0, 4 * g, corners), (FOLD_ROWS, FOLD_SLOTS + 4 * g, later)]
    if LIVE_UNITS[k] == DIAG_B:
        return [(0, SLOTS + 4 * g, corners)]
    return [(0, ROWS, corners)]


def tile_trittentioncube_pb_kernel(tc, a_heads, step2, v_pairs, W_out, b_out, out):
    nc = tc.nc
    v_plane = v_pairs.rearrange("n (p q) f -> n p q f", q=P)
    diag_col = 4 * LIVE

    with ExitStack() as stack:
        stack.enter_context(tc.manual_schedule())
        keep = stack.enter_context(tc.tile_pool(name="keep", bufs=1))
        stream = stack.enter_context(tc.tile_pool(name="stream", bufs=3))
        codes_pool = stack.enter_context(tc.tile_pool(name="codes_pool", bufs=12))
        e_pool = stack.enter_context(tc.tile_pool(name="e_pool", bufs=3))

        a_t = keep.tile([P, HEADS, P], BF16)
        s2 = keep.tile([P, P, P], BF16)
        w_codes = keep.tile([P, 512], U32, align_bytes=64)
        w_scales = keep.tile([P, 512], U8, align_bytes=64)
        bias_rows = keep.tile([P, 512], BF16)
        d_kept = [keep.tile([P, 6 * PASS + 8 * 32], F32, name="d_kept%d" % k) for k in range(2)]
        part_max = keep.tile([P, HEADS, diag_col + 1], F32)
        sums = keep.tile([P, HEADS, LIVE + 1], F32)
        const_sum = keep.tile([P, HEADS], F32)
        top = keep.tile([P, HEADS], F32)
        neg_m = keep.tile([P, HEADS], F32)
        total = keep.tile([P, HEADS], F32)
        recip = keep.tile([P, HEADS], F32)
        fill_col = keep.tile([P, 1], F32)
        warm = keep.tile([P, 1], F32)
        go = keep.tile([P, HEADS * LIVE], F32)
        live = keep.tile([P, 64], F32)
        dead = keep.tile([P, 64], F32)
        diag_s = keep.tile([P, HEADS, 8, 64], F32)
        z_bf = keep.tile([P, HEADS * P], BF16)
        o_sb = keep.tile([P, 512], F32)

        ident_bf = keep.tile([P, P], BF16)
        make_identity(nc, ident_bf)
        ident_f32 = keep.tile([P, P], F32)
        make_identity(nc, ident_f32)
        for k in range(2):
            nc.gpsimd.memset(d_kept[k], FILL)
        nc.vector.memset(fill_col, FILL)
        nc.vector.memset(part_max, FILL)
        nc.scalar.activation(out=warm, in_=fill_col, func=ACT.Exp)
        nc.vector.memset(live, 0.0)
        nc.vector.memset(dead, FILL)
        for t in range(1, 4):
            for cells, value in ((live, 1.0), (dead, 0.0)):
                nc.vector.memset(
                    cells.rearrange("r (u i b e) -> r u i b e", u=2, i=4, b=4)[:, t // 2, 0:t, :, t % 2], value
                )

        v_order = [(n, j) for n in range(HEADS) for j in range(len(V_UNITS))]
        v_raw = {}
        v_grouped = {}
        v_codes = {}

        def load_v(k):
            if k < len(v_order):
                n, j = v_order[k]
                v_raw[k] = stream.tile([P, SLOTS, P], BF16, name="v_raw", bufs=V_RAW)
                for b, (p0, q0) in enumerate(V_UNITS[j]):
                    if V_UNITS[j] == DIAG_A:
                        for fold in range(2):
                            q1 = q0 + FOLD_SLOTS * fold
                            for part in range(2):
                                p1 = p0 + FOLD_ROWS * part
                                nc.sync.dma_start(
                                    out=v_raw[k][64 * fold + b : 64 * fold + 64 : 4, FOLD_SLOTS * part : FOLD_SLOTS * (part + 1), :],
                                    in_=v_plane[n, p1 : p1 + FOLD_ROWS, q1 : q1 + FOLD_SLOTS, :],
                                )
                    else:
                        nc.sync.dma_start(out=v_raw[k][b:P:4, :, :], in_=v_plane[n, p0 : p0 + ROWS, q0 : q0 + SLOTS, :])

        def regroup_by_copy(k, first, last, copy):
            if first < last:
                copy(
                    out=v_grouped[k][:, :, first:last].rearrange("x g (c i) t -> x g c t i", i=4),
                    in_=v_raw[k][:, :, first:last].rearrange("x (g t) (c i) -> x g c t i", t=4, i=4),
                )

        def group_tile(k):
            v_grouped[k] = stream.tile([P, QUADS, P, 4], BF16, align_bytes=64, name="v_grouped", bufs=5)

        def quantise_v(k):
            n, j = v_order[k]
            codes = codes_pool.tile([P, QUADS * P], U32, align_bytes=64, name="v_codes")
            scales = codes_pool.tile([P, QUADS * P], U8, align_bytes=64, name="v_scales")
            nc.vector.quantize_mx(
                out=codes.bitcast(FP8X4), scales=scales, in_=v_grouped[k].rearrange("x g f t -> x (g f t)")
            )
            v_codes[n, j] = (codes, scales)


        with tc.tile_pool(name="early", bufs=1) as early, tc.psum_pool(name="ps_early", bufs=1) as ps_early:
            a_rows = early.tile([P, HEADS * P], BF16)
            nc.sync.dma_start(out=a_rows, in_=a_heads.rearrange("p n i -> p (n i)"))
            for k in range(V_FIRST):
                load_v(k)
            s_raw = early.tile([P, P, P], BF16)
            for rc in range(8):
                r_cols = slice(16 * rc, 16 * rc + 16)
                nc.sync.dma_start(out=s_raw[:, r_cols, :], in_=step2[r_cols].rearrange("r i q -> i r q"))
            for k in range(V_FIRST, V_RAW):
                load_v(k)

            a_ps = ps_early.tile([P, HEADS, P], BF16)
            w_bank = ps_early.tile([P, 32, 16], F32)
            for n in range(HEADS):
                nc.tensor.transpose(a_ps[:, n, :], a_rows[:, n * P : (n + 1) * P], ident_bf)
            nc.vector.tensor_copy(out=a_t, in_=a_ps)

            cut = 20
            for rc in range(8):
                r_cols = slice(16 * rc, 16 * rc + 16)
                src = s_raw[:, r_cols, :].rearrange("i r (c q) -> i c r q", q=4)
                dst = s2[:, :, r_cols].rearrange("i (c q) r -> i c r q", q=4)
                nc.vector.tensor_copy(out=dst[:, 0:cut], in_=src[:, 0:cut])
                nc.scalar.copy(out=dst[:, cut : P // 4], in_=src[:, cut : P // 4])
                if rc >= 8 - WARM_PIECES:
                    for turn in range(WARM_MATMULS):
                        nc.tensor.matmul(
                            out=w_bank, lhsT=ident_bf, rhs=s2[:, 0:32, r_cols], start=True, stop=True
                        )
                if rc % 2 == 1 and rc // 2 < V_FIRST:
                    k = rc // 2
                    group_tile(k)
                    regroup_by_copy(k, 0, 64, nc.vector.tensor_copy)
                    regroup_by_copy(k, 64, P, nc.scalar.copy)
                if rc % 2 == 0 and 0 < rc // 2 <= V_FIRST:
                    quantise_v(rc // 2 - 1)

        kept = stack.enter_context(tc.tile_pool(name="kept", bufs=5))
        ps_s = stack.enter_context(tc.psum_pool(name="ps_s", bufs=4))
        ps_t = stack.enter_context(tc.psum_pool(name="ps_t", bufs=3))
        ps_z = stack.enter_context(tc.psum_pool(name="ps_z", bufs=1))

        s_kept = {}

        def scores_and_maximum(n, k):
            if k < FOLDED:
                s_kept[n, k] = kept.tile([P, UNIT], F32, name="s_kept")
            elif k == FOLDED:
                s_kept[n, k] = d_kept[n % 2][:, 0 : 2 * PASS]
            else:
                s_kept[n, k] = d_kept[n % 2][:, 2 * PASS : 6 * PASS]
            if k == FOLDED:
                diagonal_maximum(n)
            for g in range(LIVE_PASSES[k]):
                s_ps = ps_s.tile([P, PASS], F32, name="s_ps")
                cells = s_ps.rearrange("r (u b e i) -> r u b e i", u=2, b=4, e=2)
                for part, (i0, rows, corners) in enumerate(live_parts(k, g)):
                    if rows > 0:
                        for t in range(4):
                            b = 0
                            while b < 4:
                                p0, q0 = corners[b]
                                wide = 2 if rows == ROWS and b < 3 and corners[b + 1] == (p0 + ROWS, q0) else 1
                                nc.tensor.matmul(
                                    out=cells[:, t // 2, b : b + wide, t % 2, i0 : i0 + rows],
                                    lhsT=s2[:, q0 + t, :],
                                    rhs=a_t[:, n, p0 : p0 + wide * rows].rearrange("i (b p) -> i b p", b=wide),
                                    start=True,
                                    stop=True,
                                )
                                b += wide
                for part, (i0, rows, corners) in enumerate(live_parts(k, g)):
                    if rows > 0:
                        column = 4 * k + 2 * part + g
                        nc.vector.tensor_scalar(
                            out=s_kept[n, k][:, g * PASS : (g + 1) * PASS]
                            .rearrange("r (u i c) -> r u i c", u=2, c=8)[:, :, i0 : i0 + rows, :],
                            in0=s_ps.rearrange("r (u c i) -> r u i c", u=2, c=8)[:, :, i0 : i0 + rows, :],
                            scalar1=1.0,
                            scalar2=None,
                            op0=ALU.mult,
                            op1=ALU.max,
                            accum_out=part_max[:, n, column : column + 1],
                        )

        def diagonal_of(n):
            nc.gpsimd.tensor_tensor(
                out=diag_s[:, n], in0=diag_s[:, n], in1=live.unsqueeze(1).to_broadcast([P, 8, 64]), op=ALU.mult
            )
            for j, count, first in ((0, 2, 0), (2, 2, 128 + 64), (4, 4, 2 * PASS + 128)):
                nc.gpsimd.tensor_tensor(
                    out=d_kept[n % 2][:, first : first + count * (PASS + 32)]
                    .rearrange("r (g y) -> r g y", g=count)[:, :, 0:PASS]
                    .rearrange("r g (u x) -> r g u x", u=2)[:, :, :, 0:32],
                    in0=diag_s[:, n, j : j + count].rearrange("r g (u x) -> r g u x", u=2),
                    in1=dead.rearrange("r (u x) -> r u x", u=2).unsqueeze(1).to_broadcast([P, count, 2, 32]),
                    op=ALU.add,
                )

        def diagonal_maximum(n):
            nc.vector.tensor_reduce(
                out=part_max[:, n, diag_col : diag_col + 1],
                in_=diag_s[:, n].rearrange("r s x -> r (s x)"),
                axis=AX.X,
                op=ALU.max,
            )

        def maximum_of(n):
            one = slice(n, n + 1)
            nc.vector.tensor_reduce(out=top[:, one], in_=part_max[:, n, :], axis=AX.X, op=ALU.max)
            nc.gpsimd.tensor_scalar(
                out=neg_m[:, one], in0=top[:, one], scalar1=-INV_DH, scalar2=0.0, op0=ALU.mult, op1=ALU.add
            )

        e_rows = {}
        e_grouped = {}
        e_codes = {}
        z_ps = {}

        def exp_const(n):
            e_rows[n, -1] = e_pool.tile([P, CONST], BF16, name="e_const_rows", bufs=1)
            nc.scalar.activation(
                out=e_rows[n, -1],
                in_=fill_col.to_broadcast([P, CONST]),
                func=ACT.Exp,
                bias=neg_m[:, n : n + 1],
                scale=INV_DH,
                accum_out=const_sum[:, n : n + 1],
            )

        def exp_stage(n, k):
            e_rows[n, k] = e_pool.tile([P, UNIT], BF16, name="e_rows")
            nc.scalar.activation(
                out=e_rows[n, k][:, 0 : LIVE_PASSES[k] * PASS],
                in_=s_kept[n, k],
                func=ACT.Exp,
                bias=neg_m[:, n : n + 1],
                scale=INV_DH,
                accum_out=sums[:, n, k : k + 1],
            )

        def transpose_rows(words, count, shared):
            grouped = e_pool.tile([P, UNIT], BF16, align_bytes=64, name="e_grouped")
            grouped_words = grouped.bitcast(F32).rearrange("x (g r u) -> x g r u", g=QUADS, u=2)
            for first in range(0, count, 2):
                pair = min(2, count - first)
                t_ps = ps_t.tile([P, PASS], F32, name="t_ps").rearrange("x (g u r) -> x g u r", g=2, u=2)
                for g in range(pair):
                    for u in range(2):
                        start_word = 256 * (first + g) + P * u
                        nc.tensor.transpose(t_ps[:, g, u, :], words[:, start_word : start_word + P], ident_f32)
                copy = nc.vector.tensor_copy if shared and first > 0 else nc.scalar.copy
                copy(out=grouped_words[:, first : first + pair], in_=t_ps[:, 0:pair].rearrange("x g u r -> x g r u"))
            return grouped

        def transpose_const(n):
            grouped = e_pool.tile([P, PASS], BF16, align_bytes=64, name="e_const_grouped", bufs=1)
            t_ps = ps_t.tile([P, PASS], F32, name="t_ps").rearrange("x (g u r) -> x g u r", g=2, u=2)
            nc.tensor.transpose(t_ps[:, 0, 0, :], e_rows[n, -1].bitcast(F32).to_broadcast([P, P]), ident_f32)
            nc.scalar.copy(
                out=grouped.bitcast(F32).rearrange("x (r u) -> x r u", u=2),
                in_=t_ps[:, 0, 0, :].unsqueeze(2).to_broadcast([P, P, 2]),
            )
            return grouped

        def quantise_rows(grouped, count):
            codes = e_pool.tile([P, QUADS * P], U32, align_bytes=64, name="e_codes")
            scales = e_pool.tile([P, QUADS * P], U8, align_bytes=64, name="e_scales")
            nc.vector.quantize_mx(
                out=codes[:, 0 : count * P].bitcast(FP8X4),
                scales=scales[:, 0 : count * P],
                in_=grouped[:, 0 : count * PASS],
            )
            return codes, scales

        def quantise_const(grouped):
            codes = e_pool.tile([P, 2 * P], U32, align_bytes=64, name="e_const_codes", bufs=2)
            scales = e_pool.tile([P, 2 * P], U8, align_bytes=64, name="e_const_scales", bufs=2)
            for copy in range(2):
                cols = slice(copy * P, (copy + 1) * P)
                nc.vector.quantize_mx(out=codes[:, cols].bitcast(FP8X4), scales=scales[:, cols], in_=grouped)
            return codes, scales

        def add_pass(n, e_pair, g, v_pair, h, first, last):
            nc.tensor.matmul_mx(
                out=z_ps[n],
                lhsT=e_pair[0][:, g * P : (g + 1) * P].bitcast(FP8X4),
                lhsT_scale=e_pair[1][:, g * P : (g + 1) * P],
                rhs=v_pair[0][:, h * P : (h + 1) * P].bitcast(FP8X4),
                rhs_scale=v_pair[1][:, h * P : (h + 1) * P],
                start=first,
                stop=last,
            )

        def multiply_stage(n, k):
            if k == 0:
                z_ps[n] = ps_z.tile([P, P], F32, name="z_ps")
                for j in range(MASKS):
                    for h in range(QUADS):
                        add_pass(n, e_codes[n, -1], h % 2, v_codes[n, j], h, j == 0 and h == 0, False)
            for g in range(QUADS):
                if g < LIVE_PASSES[k]:
                    add_pass(n, e_codes[n, k], g, v_codes[n, MASKS + k], g, False, k == LIVE - 1 and g == QUADS - 1)
                else:
                    add_pass(n, e_codes[n, -1], g % 2, v_codes[n, MASKS + k], g, False, False)

        def masked_sum(n):
            nc.gpsimd.tensor_scalar(
                out=sums[:, n, LIVE : LIVE + 1],
                in0=const_sum[:, n : n + 1],
                scalar1=float(MASKED_PAIRS // CONST),
                scalar2=0.0,
                op0=ALU.mult,
                op1=ALU.add,
            )

        def finish_head(n):
            nc.scalar.activation(
                out=z_bf[:, n * P : (n + 1) * P], in_=z_ps[n], func=ACT.Copy, scale=recip[:, n : n + 1]
            )

        for v in range(V_FIRST):
            load_v(v + V_RAW)
        for k in range(LIVE):
            scores_and_maximum(0, k)
            if k < V_NEXT:
                v = V_FIRST + k
                group_tile(v)
                regroup_by_copy(v, 0, P, nc.scalar.copy)
                load_v(v + V_RAW)
            if k < 2:
                for bank in range(2 * k, 2 * k + 2):
                    d_ps = ps_t.tile([P, PASS], F32, name="t_ps")
                    d_cells = d_ps.rearrange("r (n s u i b e) -> r n s u i b e", n=HEADS, s=2, u=2, i=4, b=4)
                    for s_in in range(2):
                        for b in range(4):
                            corner = ROWS * b + 4 * (2 * bank + s_in)
                            for t in range(4):
                                nc.tensor.matmul(
                                    out=d_cells[:, :, s_in, t // 2, :, b, t % 2],
                                    lhsT=s2[:, corner + t, :],
                                    rhs=a_t[:, :, corner : corner + 4],
                                    start=True,
                                    stop=True,
                                )
                    nc.scalar.copy(
                        out=diag_s[:, :, 2 * bank : 2 * bank + 2, :].rearrange("r n s x -> r n (s x)"),
                        in_=d_ps.rearrange("r (n x) -> r n x", n=HEADS),
                    )
            if k == 1:
                for n in range(2):
                    diagonal_of(n)
        maximum_of(0)
        next_v = V_FIRST + V_NEXT
        scores_and_maximum(1, 0)
        for v in range(V_FIRST, next_v - 1):
            quantise_v(v)

        units = [(n, k) for n in range(HEADS) for k in range(LIVE)]
        for i in range(len(units) + 3):
            if 0 <= i - 4 and units[i - 4][1] == LIVE - 1:
                finish_head(units[i - 4][0])
            if i < len(units):
                n, k = units[i]
                if k == 0:
                    exp_const(n)
                exp_stage(n, k)
            v_now = range(next_v, max(next_v, min(len(v_order), V_FIRST + V_NEXT + (i + 1) * V_NUM // V_DEN)))
            next_v += len(v_now)
            gp = GP if i + LIVE + 1 < len(units) else 0
            cut = CUT_LAST if i >= len(units) - LIVE else CUT
            if 0 <= i - 2 < len(units):
                n, k = units[i - 2]
                if k == 0:
                    e_codes[n, -1] = quantise_const(e_grouped[n, -1])
                one = slice(n, n + 1)
                if k == 1:
                    masked_sum(n)
                if k == LIVE - 1:
                    nc.vector.tensor_reduce(out=total[:, one], in_=sums[:, n, :], axis=AX.X, op=ALU.add)
                e_codes[n, k] = quantise_rows(e_grouped[n, k], LIVE_PASSES[k])
                if k == LIVE - 1:
                    nc.vector.reciprocal(out=recip[:, one], in_=total[:, one])
            if 0 <= i - 1 < len(units):
                n, k = units[i - 1]
                if k == 0:
                    e_grouped[n, -1] = transpose_const(n)
                e_grouped[n, k] = transpose_rows(e_rows[n, k].bitcast(F32), LIVE_PASSES[k], SHARED and n == HEADS - 1)
            for v in v_now:
                group_tile(v)
                regroup_by_copy(v, cut, P - gp, nc.scalar.copy)
            if 0 <= i - 3:
                multiply_stage(*units[i - 3])
            if i + LIVE + 1 < len(units):
                if gp > 0 and len(v_now) > 0:
                    nc.vector.memset(go[:, i : i + 1], 1.0)
                    for v in v_now:
                        nc.gpsimd.tensor_scalar(
                            out=v_grouped[v][:, :, P - gp : P, :],
                            in0=v_raw[v][:, :, P - gp : P].rearrange("x (g t) f -> x g f t", t=4),
                            scalar1=go[:, i : i + 1],
                            scalar2=0.0,
                            op0=ALU.mult,
                            op1=ALU.add,
                        )
                n, k = units[i + LIVE + 1]
                scores_and_maximum(n, k)
            if i % LIVE == LIVE - 1 and i // LIVE + 2 < HEADS:
                diagonal_of(i // LIVE + 2)
            for v in v_now:
                regroup_by_copy(v, 0, cut, nc.vector.tensor_copy)
                quantise_v(v - 1)
                load_v(v + V_RAW)
                if v == len(v_order) - 1:
                    quantise_v(v)
            if i + LIVE + 1 < len(units) and units[i + LIVE + 1][1] == LIVE - 1:
                maximum_of(units[i + LIVE + 1][0])
            if i == 0:
                w_rows = stream.tile([P, 4, 512], BF16, name="w_rows", bufs=1)
                nc.sync.dma_start(out=w_rows, in_=W_out.rearrange("(c o) k -> o c k", o=P))
            if i == W_ROUND:
                w_words = w_rows.bitcast(F32)
                w_grouped = e_pool.tile([P, UNIT], BF16, align_bytes=64, name="e_grouped")
                w_grouped_words = w_grouped.bitcast(F32).rearrange("x (c o u) -> x c o u", c=4, u=2)
                for half in range(2):
                    w_ps = ps_t.tile([P, PASS], F32, name="t_ps").rearrange("x (g u r) -> x g u r", g=2, u=2)
                    for c in range(2):
                        for u in range(2):
                            nc.tensor.transpose(w_ps[:, c, u, :], w_words[:, 2 * half + c, u * P : (u + 1) * P], ident_f32)
                    nc.vector.tensor_copy(
                        out=w_grouped_words[:, 2 * half : 2 * half + 2], in_=w_ps.rearrange("x c u o -> x c o u")
                    )
                nc.vector.quantize_mx(out=w_codes.bitcast(FP8X4), scales=w_scales, in_=w_grouped)
                nc.sync.dma_start(out=bias_rows, in_=b_out.partition_broadcast(P))

        finish_head(HEADS - 1)
        z_codes, z_scales = quantise_rows(transpose_rows(z_bf.bitcast(F32), 1, False), 1)
        o_ps = ps_s.tile([P, 512], F32, name="s_ps")
        nc.tensor.matmul_mx(
            out=o_ps,
            lhsT=z_codes[:, 0:P].bitcast(FP8X4),
            lhsT_scale=z_scales[:, 0:P],
            rhs=w_codes.bitcast(FP8X4),
            rhs_scale=w_scales,
            start=True,
            stop=True,
        )
        nc.vector.tensor_tensor(out=o_sb, in0=o_ps, in1=bias_rows, op=ALU.add)
        nc.sync.dma_start(out=out, in_=o_sb)
